import numpy as np
import ml_dtypes


def mxq(x, axis, fmt="e4m3"):
    dtype, down = {"e4m3": (ml_dtypes.float8_e4m3fn, 7), "e5m2": (ml_dtypes.float8_e5m2, 14)}[fmt]
    v = np.moveaxis(np.asarray(x, np.float32).astype(ml_dtypes.bfloat16).astype(np.float64), axis, -1)
    blocks = v.reshape(v.shape[:-1] + (-1, 32))
    amax = np.abs(blocks).max(-1, keepdims=True)
    byte = np.maximum(np.where(amax > 0, np.frexp(amax)[1] - 1 + 127, 0) - down, 1)
    scale = np.exp2(byte - 127.0)
    codes = (blocks / scale).astype(np.float32).astype(dtype).astype(np.float64)
    return np.moveaxis((codes * scale).reshape(v.shape), -1, axis)


WIDE = False


def mx_kscale(k):
    if not WIDE:
        return np.ones(k)
    levels = np.array([10, -10, 5, -5, 0])
    a = np.random.permutation(np.resize(levels, k // 512 * 4)).reshape(k // 512, 4)
    idx = np.arange(k)
    return np.exp2(a[idx // 512, idx % 128 // 32])


BF16 = ml_dtypes.bfloat16


def bf(x):
    return np.asarray(x, np.float32).astype(BF16)


def f64(x):
    return np.asarray(x).astype(np.float64)


B, C_IN, C_OUT, K, H, W = 4, 1024, 256, 3, 32, 32


def _shift2d(x, dh, dw):
    hh, ww = x.shape[2], x.shape[3]
    ph, pw = abs(dh), abs(dw)
    xp = np.pad(x, ((0, 0), (0, 0), (ph, ph), (pw, pw)))
    return xp[:, :, ph + dh: ph + dh + hh, pw + dw: pw + dw + ww]


def setup_inputs():
    s = mx_kscale(C_IN)
    bound = np.sqrt(2.0) * np.sqrt(3.0 / (C_IN * K))
    return {"x": bf(np.random.standard_normal((B, C_IN, H, W)) * s[None, :, None, None]),
            "weight": bf(np.random.uniform(-bound, bound, (C_OUT, C_IN, K)) / s[None, :, None]),
            "dilation": 1, "step": 1}


def reference(x, weight, dilation, step):
    nb, nc_in, nh, nw = x.shape
    no, nk = weight.shape[0], weight.shape[2]
    c0 = nk // 2
    xq = mxq(f64(x).reshape(nb, nc_in, nh * nw), 1, "e4m3")
    out = np.zeros((nb, no, nh, nw))
    for k in range(nk):
        off = k - c0
        y = mxq(f64(weight)[:, :, k], 1, "e4m3") @ xq
        out = out + _shift2d(y.reshape(nb, no, nh, nw), off * step, off * dilation)
    return out

@@ -1,0 +1,227 @@
+from contextlib import ExitStack
+
+import concourse.bass as bass
+import concourse.mybir as mybir
+import concourse.tile as tile
+from concourse.masks import make_identity
+
+FP8X4 = mybir.dt.float8_e4m3fn_x4
+BF16 = mybir.dt.bfloat16
+F32 = mybir.dt.float32
+U32 = mybir.dt.uint32
+U8 = mybir.dt.uint8
+
+FLOPS = 2 * 4 * 1024 * 1024 * 256 * 3
+
+P = 128
+NCOL = 4480
+FIRST = (65, 2240)
+WIN0 = (64, 2240)
+PAIR = 1120
+SHIFT = ((2240, 0, 2176), (-2176, 0, -2240))
+STORES = {0: ((0, 18, 32),), 1: ((0, 2, 18),), 2: ((0, 0, 2), (1, 20, 32)), 3: ((1, 4, 20),), 4: ((1, 0, 4),)}
+
+
+def rows(ap2d, total, start, n, pitch, width):
+    if n == 1:
+        return ap2d[:, start:start + width].rearrange("p (a c) -> p a c", a=1)
+    if start + n * pitch <= total:
+        return ap2d[:, start:start + n * pitch].rearrange("p (a c) -> p a c", c=pitch)[:, :, 0:width]
+    lead = pitch - width
+    return ap2d[:, start - lead:start - lead + n * pitch].rearrange("p (a c) -> p a c", c=pitch)[:, :, lead:pitch]
+
+
+def down(first, n):
+    last = first - n
+    return slice(first, last if last >= 0 else None, -1)
+
+
+def pieces(r, wst, n):
+    res = []
+    for pi in range(2):
+        base = FIRST[r] + PAIR * pi
+        lo = max(wst - base, 0)
+        hi = min(wst + n - base, 1056)
+        if lo >= hi:
+            continue
+        full = []
+        for s in range(lo // 33, (hi - 1) // 33 + 1):
+            w0 = max(lo - 33 * s, 0)
+            w1 = min(hi - 33 * s, 32)
+            if w1 <= w0:
+                continue
+            if w0 == 0 and w1 == 32:
+                full.append(s)
+            else:
+                res.append((pi, s, 1, w0, w1))
+        for b2 in range(2):
+            ss = [s for s in full if s % 2 == b2]
+            if ss:
+                res.append((pi, ss[0], len(ss), 0, 32))
+    return res
+
+
+def tile_skeletonconv_t_kernel(tc, x, weight, dilation, step, out):
+    nc = tc.nc
+    assert dilation == 1 and step == 1
+    with ExitStack() as ctx:
+        keep = ctx.enter_context(tc.tile_pool(name="keep", bufs=1))
+        rawp = ctx.enter_context(tc.tile_pool(name="rawp", bufs=5))
+        psp = ctx.enter_context(tc.psum_pool(name="psp", bufs=1))
+
+        ident = keep.tile([P, P], F32, name="ident")
+        make_identity(nc, ident[:])
+        ps = psp.tile([P, 4096], F32, name="ps")
+
+        grp = [keep.tile([P, 4 * NCOL], BF16, name="grp%d" % g, align_bytes=64) for g in range(2)]
+        xc = [keep.tile([P, NCOL], U32, name="xc%d" % g, align_bytes=64) for g in range(2)]
+        xs = [keep.tile([P, NCOL], U8, name="xs%d" % g, align_bytes=64) for g in range(2)]
+        wraw = [keep.tile([P, 3072], BF16, name="wraw%d" % g) for g in range(2)]
+        wsort = [keep.tile([P, 3072], BF16, name="wsort%d" % g) for g in range(2)]
+        wgrp = [keep.tile([P, 3072], BF16, name="wgrp%d" % g, align_bytes=64) for g in range(2)]
+        wc = [keep.tile([P, 768], U32, name="wc%d" % g, align_bytes=64) for g in range(2)]
+        ws = [keep.tile([P, 768], U8, name="ws%d" % g, align_bytes=64) for g in range(2)]
+        osb = [keep.tile([P, 4096], F32, name="osb%d" % m) for m in range(2)]
+
+        for g in range(2):
+            for (c0, c1) in ((0, 68), (1118, 1188), (3293, 3363), (4412, 4480)):
+                nc.vector.memset(grp[g][:, 4 * c0:4 * c1], 0.0)
+            for r in range(2):
+                for pi in range(2):
+                    sep = FIRST[r] + PAIR * pi + 32
+                    nc.vector.memset(rows(grp[g][:], 4 * NCOL, 4 * (sep - 3), 32, 132, 28), 0.0)
+
+        for g in range(2):
+            for m in range(2):
+                nc.sync.dma_start(
+                    out=wraw[g][:, m * 1536:(m + 1) * 1536],
+                    in_=weight[m * P:(m + 1) * P, g * 512:(g + 1) * 512, :].rearrange("o c k -> o (c k)"),
+                )
+        raw = {}
+        for (b, g) in ((0, 0), (1, 0), (0, 1), (1, 1), (2, 0), (3, 0), (2, 1), (3, 1)):
+            t = rawp.tile([P, 4096], BF16, name="raw")
+            nc.sync.dma_start(out=t[:], in_=x[b, g * 512:(g + 1) * 512, :, :].rearrange("(p j) h w -> p (j h w)", j=4))
+            raw[(b, g)] = t
+
+        for g in range(2):
+            for m in range(2):
+                nc.vector.tensor_copy(
+                    out=wsort[g][:, m * 1536:(m + 1) * 1536].rearrange("o (k u p e) -> o k u p e", k=3, u=2, e=2),
+                    in_=wraw[g][:, m * 1536:(m + 1) * 1536].rearrange("o (p u e k) -> o k u p e", u=2, e=2, k=3),
+                )
+            wsf = wsort[g][:].bitcast(F32)
+            wgf = wgrp[g][:].bitcast(F32)
+            for k in range(3):
+                bank = 3 * g + k
+                for m in range(2):
+                    for u in range(2):
+                        nc.tensor.transpose(
+                            ps[:, bank * 512 + m * 256 + u * P:bank * 512 + m * 256 + (u + 1) * P],
+                            wsf[:, (m * 3 + k) * 256 + u * P:(m * 3 + k) * 256 + (u + 1) * P],
+                            ident[:],
+                        )
+                nc.scalar.copy(
+                    out=wgf[:, k * 512:(k + 1) * 512].rearrange("p (n o u) -> p n o u", n=2, u=2),
+                    in_=ps[:, bank * 512:(bank + 1) * 512].rearrange("p (n u o) -> p n o u", n=2, u=2),
+                )
+            for (c0, c1) in ((0, 512), (512, 768)):
+                nc.vector.quantize_mx(
+                    out=wc[g][:, c0:c1].bitcast(FP8X4), scales=ws[g][:, c0:c1], in_=wgrp[g][:, 4 * c0:4 * c1]
+                )
+
+        def regroup(b, g, r, kap, on_scalar):
+            a0 = 8 * kap
+            base = 4 * (FIRST[r] + PAIR * (b // 2) + 33 * (b % 2) + 66 * a0)
+            dst = rows(grp[g][:], 4 * NCOL, base, 8, 264, 128)
+            src = raw[(b, g)][:].rearrange("p (j a r w) -> p j a r w", j=4, a=16, r=2)[:, :, down(15 - a0, 8), r, :]
+            if on_scalar:
+                nc.scalar.copy(
+                    out=dst.rearrange("p a (w j) -> p a w j", j=4), in_=src.rearrange("p j a w -> p a w j")
+                )
+            else:
+                nc.vector.tensor_copy(
+                    out=dst.rearrange("p a (c i j) -> p a c j i", i=4, j=4),
+                    in_=src.rearrange("p j a (c i) -> p a c j i", i=4),
+                )
+
+        def quant(g, c0, c1):
+            nc.vector.quantize_mx(
+                out=xc[g][:, c0:c1].bitcast(FP8X4), scales=xs[g][:, c0:c1], in_=grp[g][:, 4 * c0:4 * c1]
+            )
+
+        def prepare(pi, g):
+            for b in (2 * pi, 2 * pi + 1):
+                for (r, kap) in ((1, 0), (0, 0), (0, 1), (1, 1)):
+                    regroup(b, g, r, kap, (r, kap) == (1, 1))
+            if pi == 0:
+                chunks = ((0, 64), (64, 576), (2240, 2752), (2752, 3264), (576, 1088), (3264, 3328))
+            else:
+                chunks = ((1088, 1600), (3328, 3840), (3840, 4352), (1600, 2112), (2112, 2240), (4352, 4480))
+            for (c0, c1) in chunks:
+                quant(g, c0, c1)
+
+        def passes(r, i, m, g, col, first, last):
+            n = 512 if i < 4 else 128
+            wst = WIN0[r] + 512 * i
+            for k in range(3):
+                q = 2 * k + m
+                s = wst + SHIFT[r][k]
+                nc.tensor.matmul_mx(
+                    out=ps[:, col:col + n],
+                    lhsT=wc[g][:, q * P:(q + 1) * P].bitcast(FP8X4),
+                    lhsT_scale=ws[g][:, q * P:(q + 1) * P],
+                    rhs=xc[g][:, s:s + n].bitcast(FP8X4),
+                    rhs_scale=xs[g][:, s:s + n],
+                    start=(first and k == 0),
+                    stop=(last and k == 2),
+                )
+
+        def drain(r, i, m, col):
+            n = 512 if i < 4 else 128
+            wst = WIN0[r] + 512 * i
+            ov = osb[m][:].rearrange("p (b a r w) -> p b a r w", b=4, a=16, r=2)
+            for (pi, s0, ns, w0, w1) in pieces(r, wst, n):
+                j0 = col + FIRST[r] + PAIR * pi + 33 * s0 + w0 - wst
+                nc.scalar.copy(
+                    out=ov[:, 2 * pi + s0 % 2, down(15 - s0 // 2, ns), r, w0:w1],
+                    in_=rows(ps[:], 4096, j0, ns, 66, w1 - w0),
+                )
+
+        def store(i, m):
+            for (pi, h0, h1) in STORES[i]:
+                nc.sync.dma_start(
+                    out=out[2 * pi:2 * pi + 2, m * P:(m + 1) * P, h0:h1, :].rearrange("b o h w -> o b (h w)"),
+                    in_=osb[m][:].rearrange("p (b c) -> p b c", b=4)[:, 2 * pi:2 * pi + 2, 32 * h0:32 * h1],
+                )
+
+        def groups(i0):
+            return [(r, i, m) for (r, i) in ((1, i0), (0, i0), (1, i0 + 1), (0, i0 + 1)) for m in range(2)]
+
+        def bank_of(n):
+            return ((6 + n) % 8) * 512
+
+        prepare(0, 0)
+        for n, (r, i, m) in enumerate(groups(0)):
+            passes(r, i, m, 0, bank_of(n), True, False)
+        prepare(0, 1)
+        prepare(1, 0)
+        for n, (r, i, m) in enumerate(groups(0)):
+            passes(r, i, m, 1, bank_of(n), False, True)
+            drain(r, i, m, bank_of(n))
+            if r == 0:
+                store(i, m)
+        for n, (r, i, m) in enumerate(groups(2)):
+            passes(r, i, m, 0, bank_of(n), True, False)
+        prepare(1, 1)
+        for n, (r, i, m) in enumerate(groups(2)):
+            passes(r, i, m, 1, bank_of(n), False, True)
+            drain(r, i, m, bank_of(n))
+            if r == 0:
+                store(i, m)
+        for n, (r, m) in enumerate(((1, 0), (1, 1), (0, 0), (0, 1))):
+            col = bank_of(0) + 128 * n
+            passes(r, 4, m, 0, col, True, False)
+            passes(r, 4, m, 1, col, False, True)
+            drain(r, 4, m, col)
+            if r == 0:
+                store(4, m)

@@ -61,6 +61,13 @@ def pieces(r, wst, n):
     return res
 
 
+CHUNKS = {
+    0: (((2240, 2752), (2752, 2816)), ((0, 64), (64, 576)), ((2816, 3328), (576, 1088))),
+    1: (((3328, 3840),), ((1088, 1600),), ((3840, 4352), (1600, 2112), (4352, 4480), (2112, 2240))),
+}
+SPLIT = (8, 10)
+
+
 def tile_skeletonconv_t_kernel(tc, x, weight, dilation, step, out):
     nc = tc.nc
     assert dilation == 1 and step == 1
@@ -68,6 +75,7 @@ def tile_skeletonconv_t_kernel(tc, x, weight, dilation, step, out):
         keep = ctx.enter_context(tc.tile_pool(name="keep", bufs=1))
         rawp = ctx.enter_context(tc.tile_pool(name="rawp", bufs=5))
         psp = ctx.enter_context(tc.psum_pool(name="psp", bufs=1))
+        ctx.enter_context(tc.manual_schedule())
 
         ident = keep.tile([P, P], F32, name="ident")
         make_identity(nc, ident[:])
@@ -84,12 +92,13 @@ def tile_skeletonconv_t_kernel(tc, x, weight, dilation, step, out):
         osb = [keep.tile([P, 4096], F32, name="osb%d" % m) for m in range(2)]
 
         for g in range(2):
+            gf = grp[g][:].bitcast(F32)
             for (c0, c1) in ((0, 68), (1118, 1188), (3293, 3363), (4412, 4480)):
-                nc.vector.memset(grp[g][:, 4 * c0:4 * c1], 0.0)
+                nc.gpsimd.memset(gf[:, 2 * c0:2 * c1], 0.0)
             for r in range(2):
                 for pi in range(2):
                     sep = FIRST[r] + PAIR * pi + 32
-                    nc.vector.memset(rows(grp[g][:], 4 * NCOL, 4 * (sep - 3), 32, 132, 28), 0.0)
+                    nc.gpsimd.memset(rows(gf, 2 * NCOL, 2 * (sep - 3), 32, 66, 14), 0.0)
 
         for g in range(2):
             for m in range(2):
@@ -110,7 +119,6 @@ def tile_skeletonconv_t_kernel(tc, x, weight, dilation, step, out):
                     in_=wraw[g][:, m * 1536:(m + 1) * 1536].rearrange("o (p u e k) -> o k u p e", u=2, e=2, k=3),
                 )
             wsf = wsort[g][:].bitcast(F32)
-            wgf = wgrp[g][:].bitcast(F32)
             for k in range(3):
                 bank = 3 * g + k
                 for m in range(2):
@@ -120,20 +128,26 @@ def tile_skeletonconv_t_kernel(tc, x, weight, dilation, step, out):
                             wsf[:, (m * 3 + k) * 256 + u * P:(m * 3 + k) * 256 + (u + 1) * P],
                             ident[:],
                         )
+
+        def weights_out(g):
+            wgf = wgrp[g][:].bitcast(F32)
+            for k in range(3):
+                bank = 3 * g + k
                 nc.scalar.copy(
                     out=wgf[:, k * 512:(k + 1) * 512].rearrange("p (n o u) -> p n o u", n=2, u=2),
                     in_=ps[:, bank * 512:(bank + 1) * 512].rearrange("p (n u o) -> p n o u", n=2, u=2),
                 )
+
+        def weights_quant(g):
             for (c0, c1) in ((0, 512), (512, 768)):
                 nc.vector.quantize_mx(
                     out=wc[g][:, c0:c1].bitcast(FP8X4), scales=ws[g][:, c0:c1], in_=wgrp[g][:, 4 * c0:4 * c1]
                 )
 
-        def regroup(b, g, r, kap, on_scalar):
-            a0 = 8 * kap
+        def regroup(b, g, r, a0, a1, on_scalar):
             base = 4 * (FIRST[r] + PAIR * (b // 2) + 33 * (b % 2) + 66 * a0)
-            dst = rows(grp[g][:], 4 * NCOL, base, 8, 264, 128)
-            src = raw[(b, g)][:].rearrange("p (j a r w) -> p j a r w", j=4, a=16, r=2)[:, :, down(15 - a0, 8), r, :]
+            dst = rows(grp[g][:], 4 * NCOL, base, a1 - a0, 264, 128)
+            src = raw[(b, g)][:].rearrange("p (j a r w) -> p j a r w", j=4, a=16, r=2)[:, :, down(15 - a0, a1 - a0), r, :]
             if on_scalar:
                 nc.scalar.copy(
                     out=dst.rearrange("p a (w j) -> p a w j", j=4), in_=src.rearrange("p j a w -> p a w j")
@@ -144,37 +158,41 @@ def tile_skeletonconv_t_kernel(tc, x, weight, dilation, step, out):
                     in_=src.rearrange("p j a (c i) -> p a c j i", i=4),
                 )
 
-        def quant(g, c0, c1):
-            nc.vector.quantize_mx(
-                out=xc[g][:, c0:c1].bitcast(FP8X4), scales=xs[g][:, c0:c1], in_=grp[g][:, 4 * c0:4 * c1]
-            )
-
-        def prepare(pi, g):
-            for b in (2 * pi, 2 * pi + 1):
-                for (r, kap) in ((1, 0), (0, 0), (0, 1), (1, 1)):
-                    regroup(b, g, r, kap, (r, kap) == (1, 1))
-            if pi == 0:
-                chunks = ((0, 64), (64, 576), (2240, 2752), (2752, 3264), (576, 1088), (3264, 3328))
-            else:
-                chunks = ((1088, 1600), (3328, 3840), (3840, 4352), (1600, 2112), (2112, 2240), (4352, 4480))
+        def quant(g, chunks):
             for (c0, c1) in chunks:
-                quant(g, c0, c1)
-
-        def passes(r, i, m, g, col, first, last):
-            n = 512 if i < 4 else 128
-            wst = WIN0[r] + 512 * i
-            for k in range(3):
-                q = 2 * k + m
-                s = wst + SHIFT[r][k]
-                nc.tensor.matmul_mx(
-                    out=ps[:, col:col + n],
-                    lhsT=wc[g][:, q * P:(q + 1) * P].bitcast(FP8X4),
-                    lhsT_scale=ws[g][:, q * P:(q + 1) * P],
-                    rhs=xc[g][:, s:s + n].bitcast(FP8X4),
-                    rhs_scale=xs[g][:, s:s + n],
-                    start=(first and k == 0),
-                    stop=(last and k == 2),
+                nc.vector.quantize_mx(
+                    out=xc[g][:, c0:c1].bitcast(FP8X4), scales=xs[g][:, c0:c1], in_=grp[g][:, 4 * c0:4 * c1]
                 )
+
+        def prepare(pi, g, with_weights):
+            b0 = 2 * pi
+            regroup(b0, g, 1, 0, SPLIT[1], False)
+            regroup(b0, g, 0, 0, SPLIT[0], False)
+            if with_weights:
+                weights_quant(g)
+            regroup(b0, g, 1, SPLIT[1], 16, True)
+            regroup(b0, g, 0, SPLIT[0], 16, False)
+            regroup(b0 + 1, g, 1, 0, SPLIT[1], False)
+            quant(g, CHUNKS[pi][0])
+            regroup(b0 + 1, g, 0, 0, SPLIT[0], False)
+            quant(g, CHUNKS[pi][1])
+            regroup(b0 + 1, g, 1, SPLIT[1], 16, True)
+            regroup(b0 + 1, g, 0, SPLIT[0], 16, False)
+            quant(g, CHUNKS[pi][2])
+
+        def one_pass(r, i, m, g, k, col, start, stop):
+            n = 512 if i < 4 else 128
+            s = WIN0[r] + 512 * i + SHIFT[r][k]
+            q = 2 * k + m
+            nc.tensor.matmul_mx(
+                out=ps[:, col:col + n],
+                lhsT=wc[g][:, q * P:(q + 1) * P].bitcast(FP8X4),
+                lhsT_scale=ws[g][:, q * P:(q + 1) * P],
+                rhs=xc[g][:, s:s + n].bitcast(FP8X4),
+                rhs_scale=xs[g][:, s:s + n],
+                start=start,
+                stop=stop,
+            )
 
         def drain(r, i, m, col):
             n = 512 if i < 4 else 128
@@ -195,33 +213,38 @@ def tile_skeletonconv_t_kernel(tc, x, weight, dilation, step, out):
                 )
 
         def groups(i0):
-            return [(r, i, m) for (r, i) in ((1, i0), (0, i0), (1, i0 + 1), (0, i0 + 1)) for m in range(2)]
+            return [(r, i, m) for i in (i0, i0 + 1) for m in range(2) for r in (1, 0)]
 
         def bank_of(n):
             return ((6 + n) % 8) * 512
 
-        prepare(0, 0)
-        for n, (r, i, m) in enumerate(groups(0)):
-            passes(r, i, m, 0, bank_of(n), True, False)
-        prepare(0, 1)
-        prepare(1, 0)
-        for n, (r, i, m) in enumerate(groups(0)):
-            passes(r, i, m, 1, bank_of(n), False, True)
-            drain(r, i, m, bank_of(n))
-            if r == 0:
-                store(i, m)
-        for n, (r, i, m) in enumerate(groups(2)):
-            passes(r, i, m, 0, bank_of(n), True, False)
-        prepare(1, 1)
-        for n, (r, i, m) in enumerate(groups(2)):
-            passes(r, i, m, 1, bank_of(n), False, True)
-            drain(r, i, m, bank_of(n))
-            if r == 0:
-                store(i, m)
-        for n, (r, m) in enumerate(((1, 0), (1, 1), (0, 0), (0, 1))):
-            col = bank_of(0) + 128 * n
-            passes(r, 4, m, 0, col, True, False)
-            passes(r, 4, m, 1, col, False, True)
-            drain(r, 4, m, col)
+        def sweep(i0, g, ns):
+            for n in ns:
+                (r, i, m) = groups(i0)[n]
+                for k in range(3):
+                    one_pass(r, i, m, g, k, bank_of(n), g == 0 and k == 0, g == 1 and k == 2)
+                if g == 1:
+                    drain(r, i, m, bank_of(n))
+                    if r == 0:
+                        store(i, m)
+
+        weights_out(0)
+        prepare(0, 0, True)
+        weights_out(1)
+        for (r, k) in ((1, 1), (0, 2), (0, 0), (1, 2), (1, 0), (0, 1)):
+            for m in range(2):
+                one_pass(r, 0, m, 0, k, bank_of(groups(0).index((r, 0, m))), (r, k) in ((1, 1), (0, 2)), False)
+        sweep(0, 0, range(4, 8))
+        prepare(0, 1, True)
+        prepare(1, 0, False)
+        sweep(0, 1, range(8))
+        prepare(1, 1, False)
+        sweep(2, 0, range(8))
+        sweep(2, 1, range(8))
+        for n, (r, m) in enumerate(((1, 0), (0, 0), (1, 1), (0, 1))):
+            for g in range(2):
+                for k in range(3):
+                    one_pass(r, 4, m, g, k, bank_of(n), g == 0 and k == 0, g == 1 and k == 2)
+            drain(r, 4, m, bank_of(n))
             if r == 0:
                 store(4, m)

@@ -73,7 +73,7 @@ def tile_skeletonconv_t_kernel(tc, x, weight, dilation, step, out):
     assert dilation == 1 and step == 1
     with ExitStack() as ctx:
         keep = ctx.enter_context(tc.tile_pool(name="keep", bufs=1))
-        rawp = ctx.enter_context(tc.tile_pool(name="rawp", bufs=5))
+        rawp = ctx.enter_context(tc.tile_pool(name="rawp", bufs=7))
         psp = ctx.enter_context(tc.psum_pool(name="psp", bufs=1))
         ctx.enter_context(tc.manual_schedule())
 
@@ -81,29 +81,31 @@ def tile_skeletonconv_t_kernel(tc, x, weight, dilation, step, out):
         make_identity(nc, ident[:])
         ps = psp.tile([P, 4096], F32, name="ps")
 
-        grp = [keep.tile([P, 4 * NCOL], BF16, name="grp%d" % g, align_bytes=64) for g in range(2)]
+        grp_all = keep.tile([P, 2 * 4 * NCOL], BF16, name="grp_all", align_bytes=64)
+        grp = [grp_all[:, g * 4 * NCOL:(g + 1) * 4 * NCOL] for g in range(2)]
         xc = [keep.tile([P, NCOL], U32, name="xc%d" % g, align_bytes=64) for g in range(2)]
         xs = [keep.tile([P, NCOL], U8, name="xs%d" % g, align_bytes=64) for g in range(2)]
-        wraw = [keep.tile([P, 3072], BF16, name="wraw%d" % g) for g in range(2)]
         wsort = [keep.tile([P, 3072], BF16, name="wsort%d" % g) for g in range(2)]
         wgrp = [keep.tile([P, 3072], BF16, name="wgrp%d" % g, align_bytes=64) for g in range(2)]
         wc = [keep.tile([P, 768], U32, name="wc%d" % g, align_bytes=64) for g in range(2)]
         ws = [keep.tile([P, 768], U8, name="ws%d" % g, align_bytes=64) for g in range(2)]
         osb = [keep.tile([P, 4096], F32, name="osb%d" % m) for m in range(2)]
 
-        for g in range(2):
-            gf = grp[g][:].bitcast(F32)
-            for (c0, c1) in ((0, 68), (1118, 1188), (3293, 3363), (4412, 4480)):
-                nc.gpsimd.memset(gf[:, 2 * c0:2 * c1], 0.0)
-            for r in range(2):
-                for pi in range(2):
-                    sep = FIRST[r] + PAIR * pi + 32
-                    nc.gpsimd.memset(rows(gf, 2 * NCOL, 2 * (sep - 3), 32, 66, 14), 0.0)
+        gf = grp_all[:].bitcast(F32).rearrange("p (g c) -> p g c", g=2)
+        for (c0, c1) in ((0, 68), (1118, 1188), (3293, 3363), (4412, 4480)):
+            nc.vector.memset(gf[:, :, 2 * c0:2 * c1], 0.0)
+        for r in range(2):
+            for pi in range(2):
+                lo = 2 * (FIRST[r] + PAIR * pi + 32 - 3)
+                nc.vector.memset(gf[:, :, lo:lo + 32 * 66].rearrange("p g (a c) -> p g a c", c=66)[:, :, :, 0:14], 0.0)
 
+        wraw = []
         for g in range(2):
+            t = rawp.tile([P, 4096], BF16, name="raw")
+            wraw.append(t)
             for m in range(2):
                 nc.sync.dma_start(
-                    out=wraw[g][:, m * 1536:(m + 1) * 1536],
+                    out=t[:, m * 1536:(m + 1) * 1536],
                     in_=weight[m * P:(m + 1) * P, g * 512:(g + 1) * 512, :].rearrange("o c k -> o (c k)"),
                 )
         raw = {}
@@ -146,7 +148,7 @@ def tile_skeletonconv_t_kernel(tc, x, weight, dilation, step, out):
 
         def regroup(b, g, r, a0, a1, on_scalar):
             base = 4 * (FIRST[r] + PAIR * (b // 2) + 33 * (b % 2) + 66 * a0)
-            dst = rows(grp[g][:], 4 * NCOL, base, a1 - a0, 264, 128)
+            dst = rows(grp[g], 4 * NCOL, base, a1 - a0, 264, 128)
             src = raw[(b, g)][:].rearrange("p (j a r w) -> p j a r w", j=4, a=16, r=2)[:, :, down(15 - a0, a1 - a0), r, :]
             if on_scalar:
                 nc.scalar.copy(

@@ -93,11 +93,11 @@ def tile_skeletonconv_t_kernel(tc, x, weight, dilation, step, out):
 
         gf = grp_all[:].bitcast(F32).rearrange("p (g c) -> p g c", g=2)
         for (c0, c1) in ((0, 68), (1118, 1188), (3293, 3363), (4412, 4480)):
-            nc.vector.memset(gf[:, :, 2 * c0:2 * c1], 0.0)
+            nc.gpsimd.memset(gf[:, :, 2 * c0:2 * c1], 0.0)
         for r in range(2):
             for pi in range(2):
                 lo = 2 * (FIRST[r] + PAIR * pi + 32 - 3)
-                nc.vector.memset(gf[:, :, lo:lo + 32 * 66].rearrange("p g (a c) -> p g a c", c=66)[:, :, :, 0:14], 0.0)
+                nc.gpsimd.memset(gf[:, :, lo:lo + 32 * 66].rearrange("p g (a c) -> p g a c", c=66)[:, :, :, 0:14], 0.0)
 
         wraw = []
         for g in range(2):
@@ -168,18 +168,19 @@ def tile_skeletonconv_t_kernel(tc, x, weight, dilation, step, out):
 
         def prepare(pi, g, with_weights):
             b0 = 2 * pi
+            even_on_scalar = (pi, g) != (1, 0)
             regroup(b0, g, 1, 0, SPLIT[1], False)
             regroup(b0, g, 0, 0, SPLIT[0], False)
             if with_weights:
                 weights_quant(g)
             regroup(b0, g, 1, SPLIT[1], 16, True)
-            regroup(b0, g, 0, SPLIT[0], 16, False)
+            regroup(b0, g, 0, SPLIT[0], 16, even_on_scalar)
             regroup(b0 + 1, g, 1, 0, SPLIT[1], False)
-            quant(g, CHUNKS[pi][0])
             regroup(b0 + 1, g, 0, 0, SPLIT[0], False)
+            quant(g, CHUNKS[pi][0])
             quant(g, CHUNKS[pi][1])
             regroup(b0 + 1, g, 1, SPLIT[1], 16, True)
-            regroup(b0 + 1, g, 0, SPLIT[0], 16, False)
+            regroup(b0 + 1, g, 0, SPLIT[0], 16, even_on_scalar)
             quant(g, CHUNKS[pi][2])
 
         def one_pass(r, i, m, g, k, col, start, stop):
@@ -196,16 +197,18 @@ def tile_skeletonconv_t_kernel(tc, x, weight, dilation, step, out):
                 stop=stop,
             )
 
-        def drain(r, i, m, col):
+        def drain(r, i, m, col, on_vector):
             n = 512 if i < 4 else 128
             wst = WIN0[r] + 512 * i
             ov = osb[m][:].rearrange("p (b a r w) -> p b a r w", b=4, a=16, r=2)
             for (pi, s0, ns, w0, w1) in pieces(r, wst, n):
                 j0 = col + FIRST[r] + PAIR * pi + 33 * s0 + w0 - wst
-                nc.scalar.copy(
-                    out=ov[:, 2 * pi + s0 % 2, down(15 - s0 // 2, ns), r, w0:w1],
-                    in_=rows(ps[:], 4096, j0, ns, 66, w1 - w0),
-                )
+                dst = ov[:, 2 * pi + s0 % 2, down(15 - s0 // 2, ns), r, w0:w1]
+                src = rows(ps[:], 4096, j0, ns, 66, w1 - w0)
+                if on_vector:
+                    nc.vector.tensor_copy(out=dst, in_=src)
+                else:
+                    nc.scalar.copy(out=dst, in_=src)
 
         def store(i, m):
             for (pi, h0, h1) in STORES[i]:
@@ -226,7 +229,7 @@ def tile_skeletonconv_t_kernel(tc, x, weight, dilation, step, out):
                 for k in range(3):
                     one_pass(r, i, m, g, k, bank_of(n), g == 0 and k == 0, g == 1 and k == 2)
                 if g == 1:
-                    drain(r, i, m, bank_of(n))
+                    drain(r, i, m, bank_of(n), i0 == 2 and m == 1)
                     if r == 0:
                         store(i, m)
 
@@ -247,6 +250,6 @@ def tile_skeletonconv_t_kernel(tc, x, weight, dilation, step, out):
             for g in range(2):
                 for k in range(3):
                     one_pass(r, 4, m, g, k, bank_of(n), g == 0 and k == 0, g == 1 and k == 2)
-            drain(r, 4, m, bank_of(n))
+            drain(r, 4, m, bank_of(n), m == 1)
             if r == 0:
                 store(4, m)

@@ -176,8 +176,12 @@ def tile_skeletonconv_t_kernel(tc, x, weight, dilation, step, out):
             regroup(b0, g, 1, SPLIT[1], 16, True)
             regroup(b0, g, 0, SPLIT[0], 16, even_on_scalar)
             regroup(b0 + 1, g, 1, 0, SPLIT[1], False)
-            regroup(b0 + 1, g, 0, 0, SPLIT[0], False)
-            quant(g, CHUNKS[pi][0])
+            if (pi, g) == (0, 0):
+                quant(g, CHUNKS[pi][0])
+                regroup(b0 + 1, g, 0, 0, SPLIT[0], False)
+            else:
+                regroup(b0 + 1, g, 0, 0, SPLIT[0], False)
+                quant(g, CHUNKS[pi][0])
             quant(g, CHUNKS[pi][1])
             regroup(b0 + 1, g, 1, SPLIT[1], 16, True)
             regroup(b0 + 1, g, 0, SPLIT[0], 16, even_on_scalar)
@@ -233,6 +237,15 @@ def tile_skeletonconv_t_kernel(tc, x, weight, dilation, step, out):
                     if r == 0:
                         store(i, m)
 
+        def warm(moving, times):
+            for n in range(times):
+                nc.tensor.matmul(
+                    out=ps[:, bank_of(0):bank_of(0) + 512], lhsT=wsort[0][:, 0:P], rhs=moving[:, 0:512], start=True, stop=True
+                )
+
+        warm(wsort[1], 4)
+        warm(raw[(0, 0)], 2)
+        warm(raw[(1, 0)], 3)
         weights_out(0)
         prepare(0, 0, True)
         weights_out(1)

@@ -237,15 +237,6 @@ def tile_skeletonconv_t_kernel(tc, x, weight, dilation, step, out):
                     if r == 0:
                         store(i, m)
 
-        def warm(moving, times):
-            for n in range(times):
-                nc.tensor.matmul(
-                    out=ps[:, bank_of(0):bank_of(0) + 512], lhsT=wsort[0][:, 0:P], rhs=moving[:, 0:512], start=True, stop=True
-                )
-
-        warm(wsort[1], 4)
-        warm(raw[(0, 0)], 2)
-        warm(raw[(1, 0)], 3)
         weights_out(0)
         prepare(0, 0, True)
         weights_out(1)

@@ -117,8 +117,8 @@ def tile_skeletonconv_t_kernel(tc, x, weight, dilation, step, out):
         for g in range(2):
             for m in range(2):
                 nc.vector.tensor_copy(
-                    out=wsort[g][:, m * 1536:(m + 1) * 1536].rearrange("o (k u p e) -> o k u p e", k=3, u=2, e=2),
-                    in_=wraw[g][:, m * 1536:(m + 1) * 1536].rearrange("o (p u e k) -> o k u p e", u=2, e=2, k=3),
+                    out=wsort[g][:, m * 1536:(m + 1) * 1536].rearrange("o (k c) -> o c k", k=3),
+                    in_=wraw[g][:, m * 1536:(m + 1) * 1536].rearrange("o (c k) -> o c k", k=3),
                 )
             wsf = wsort[g][:].bitcast(F32)
             for k in range(3):
@@ -127,7 +127,7 @@ def tile_skeletonconv_t_kernel(tc, x, weight, dilation, step, out):
                     for u in range(2):
                         nc.tensor.transpose(
                             ps[:, bank * 512 + m * 256 + u * P:bank * 512 + m * 256 + (u + 1) * P],
-                            wsf[:, (m * 3 + k) * 256 + u * P:(m * 3 + k) * 256 + (u + 1) * P],
+                            wsf[:, (m * 3 + k) * 256 + u:(m * 3 + k + 1) * 256:2],
                             ident[:],
                         )
 

@@ -92,12 +92,12 @@ def tile_skeletonconv_t_kernel(tc, x, weight, dilation, step, out):
         osb = [keep.tile([P, 4096], F32, name="osb%d" % m) for m in range(2)]
 
         gf = grp_all[:].bitcast(F32).rearrange("p (g c) -> p g c", g=2)
-        for (c0, c1) in ((0, 68), (1118, 1188), (3293, 3363), (4412, 4480)):
-            nc.gpsimd.memset(gf[:, :, 2 * c0:2 * c1], 0.0)
-        for r in range(2):
-            for pi in range(2):
+        for pi in range(2):
+            for r in (1, 0):
                 lo = 2 * (FIRST[r] + PAIR * pi + 32 - 3)
                 nc.gpsimd.memset(gf[:, :, lo:lo + 32 * 66].rearrange("p g (a c) -> p g a c", c=66)[:, :, :, 0:14], 0.0)
+            for (c0, c1) in (((0, 68), (1118, 1188), (3293, 3363)), ((4412, 4480),))[pi]:
+                nc.gpsimd.memset(gf[:, :, 2 * c0:2 * c1], 0.0)
 
         wraw = []
         for g in range(2):

@@ -94,10 +94,10 @@ def tile_skeletonconv_t_kernel(tc, x, weight, dilation, step, out):
         gf = grp_all[:].bitcast(F32).rearrange("p (g c) -> p g c", g=2)
         for pi in range(2):
             for r in (1, 0):
-                lo = 2 * (FIRST[r] + PAIR * pi + 32 - 3)
-                nc.gpsimd.memset(gf[:, :, lo:lo + 32 * 66].rearrange("p g (a c) -> p g a c", c=66)[:, :, :, 0:14], 0.0)
-            for (c0, c1) in (((0, 68), (1118, 1188), (3293, 3363)), ((4412, 4480),))[pi]:
-                nc.gpsimd.memset(gf[:, :, 2 * c0:2 * c1], 0.0)
+                lo = 2 * (FIRST[r] + PAIR * pi + 32)
+                nc.vector.memset(gf[:, :, lo:lo + 32 * 66].rearrange("p g (a c) -> p g a c", c=66)[:, :, :, 0:2], 0.0)
+        for (c0, c1) in ((0, 65), (1121, 1185), (3296, 3360), (4416, 4480)):
+            nc.vector.memset(gf[:, :, 2 * c0:2 * c1], 0.0)
 
         wraw = []
         for g in range(2):

@@ -152,7 +152,8 @@ def tile_skeletonconv_t_kernel(tc, x, weight, dilation, step, out):
             src = raw[(b, g)][:].rearrange("p (j a r w) -> p j a r w", j=4, a=16, r=2)[:, :, down(15 - a0, a1 - a0), r, :]
             if on_scalar:
                 nc.scalar.copy(
-                    out=dst.rearrange("p a (w j) -> p a w j", j=4), in_=src.rearrange("p j a w -> p a w j")
+                    out=dst.rearrange("p a (c i j) -> p a c j i", i=4, j=4),
+                    in_=src.rearrange("p j a (c i) -> p a c j i", i=4),
                 )
             else:
                 nc.vector.tensor_copy(

@@ -99,162 +99,245 @@ def tile_skeletonconv_t_kernel(tc, x, weight, dilation, step, out):
         for (c0, c1) in ((0, 65), (1121, 1185), (3296, 3360), (4416, 4480)):
             nc.vector.memset(gf[:, :, 2 * c0:2 * c1], 0.0)
 
-        wraw = []
-        for g in range(2):
-            t = rawp.tile([P, 4096], BF16, name="raw")
-            wraw.append(t)
-            for m in range(2):
-                nc.sync.dma_start(
-                    out=t[:, m * 1536:(m + 1) * 1536],
-                    in_=weight[m * P:(m + 1) * P, g * 512:(g + 1) * 512, :].rearrange("o c k -> o (c k)"),
-                )
+        wraw = [rawp.tile([P, 4096], BF16, name="raw") for g in range(2)]
         raw = {}
-        for (b, g) in ((0, 0), (1, 0), (0, 1), (1, 1), (2, 0), (3, 0), (2, 1), (3, 1)):
-            t = rawp.tile([P, 4096], BF16, name="raw")
-            nc.sync.dma_start(out=t[:], in_=x[b, g * 512:(g + 1) * 512, :, :].rearrange("(p j) h w -> p (j h w)", j=4))
-            raw[(b, g)] = t
 
-        for g in range(2):
-            for m in range(2):
-                nc.vector.tensor_copy(
-                    out=wsort[g][:, m * 1536:(m + 1) * 1536].rearrange("o (k c) -> o c k", k=3),
-                    in_=wraw[g][:, m * 1536:(m + 1) * 1536].rearrange("o (c k) -> o c k", k=3),
-                )
+        def copy_on(eng, out, in_):
+            if eng == "S":
+                nc.scalar.copy(out=out, in_=in_)
+            else:
+                nc.vector.tensor_copy(out=out, in_=in_)
+
+        def load_w(g, m):
+            nc.sync.dma_start(
+                out=wraw[g][:, m * 1536:(m + 1) * 1536],
+                in_=weight[m * P:(m + 1) * P, g * 512:(g + 1) * 512, :].rearrange("o c k -> o (c k)"),
+            )
+
+        def load_x(b, g, h0=0, h1=32):
+            if (b, g) not in raw:
+                raw[(b, g)] = rawp.tile([P, 4096], BF16, name="raw")
+            nc.sync.dma_start(
+                out=raw[(b, g)][:].rearrange("p (j c) -> p j c", j=4)[:, :, 32 * h0:32 * h1],
+                in_=x[b, g * 512:(g + 1) * 512, h0:h1, :].rearrange("(p j) h w -> p j (h w)", j=4),
+            )
+
+        def wsrt(g, m, c0, c1, eng):
+            copy_on(
+                eng,
+                wsort[g][:, m * 1536:(m + 1) * 1536].rearrange("o (k c) -> o c k", k=3)[:, c0:c1, :],
+                wraw[g][:, m * 1536:(m + 1) * 1536].rearrange("o (c k) -> o c k", k=3)[:, c0:c1, :],
+            )
+
+        def wtrans(g, k, ms=(0, 1)):
             wsf = wsort[g][:].bitcast(F32)
-            for k in range(3):
-                bank = 3 * g + k
-                for m in range(2):
-                    for u in range(2):
-                        nc.tensor.transpose(
-                            ps[:, bank * 512 + m * 256 + u * P:bank * 512 + m * 256 + (u + 1) * P],
-                            wsf[:, (m * 3 + k) * 256 + u:(m * 3 + k + 1) * 256:2],
-                            ident[:],
-                        )
+            bank = 3 * g + k
+            for m in ms:
+                for u in range(2):
+                    nc.tensor.transpose(
+                        ps[:, bank * 512 + m * 256 + u * P:bank * 512 + m * 256 + (u + 1) * P],
+                        wsf[:, (m * 3 + k) * 256 + u:(m * 3 + k + 1) * 256:2],
+                        ident[:],
+                    )
 
-        def weights_out(g):
+        def wout(g, k, eng):
             wgf = wgrp[g][:].bitcast(F32)
-            for k in range(3):
-                bank = 3 * g + k
-                nc.scalar.copy(
-                    out=wgf[:, k * 512:(k + 1) * 512].rearrange("p (n o u) -> p n o u", n=2, u=2),
-                    in_=ps[:, bank * 512:(bank + 1) * 512].rearrange("p (n u o) -> p n o u", n=2, u=2),
-                )
+            bank = 3 * g + k
+            copy_on(
+                eng,
+                wgf[:, k * 512:(k + 1) * 512].rearrange("p (n o u) -> p n o u", n=2, u=2),
+                ps[:, bank * 512:(bank + 1) * 512].rearrange("p (n u o) -> p n o u", n=2, u=2),
+            )
 
-        def weights_quant(g):
-            for (c0, c1) in ((0, 512), (512, 768)):
-                nc.vector.quantize_mx(
-                    out=wc[g][:, c0:c1].bitcast(FP8X4), scales=ws[g][:, c0:c1], in_=wgrp[g][:, 4 * c0:4 * c1]
-                )
+        def wq(g, c0, c1):
+            nc.vector.quantize_mx(
+                out=wc[g][:, c0:c1].bitcast(FP8X4), scales=ws[g][:, c0:c1], in_=wgrp[g][:, 4 * c0:4 * c1]
+            )
 
-        def regroup(b, g, r, a0, a1, on_scalar):
+        def rg(b, g, r, a0, a1, eng):
             base = 4 * (FIRST[r] + PAIR * (b // 2) + 33 * (b % 2) + 66 * a0)
             dst = rows(grp[g], 4 * NCOL, base, a1 - a0, 264, 128)
             src = raw[(b, g)][:].rearrange("p (j a r w) -> p j a r w", j=4, a=16, r=2)[:, :, down(15 - a0, a1 - a0), r, :]
-            if on_scalar:
-                nc.scalar.copy(
-                    out=dst.rearrange("p a (c i j) -> p a c j i", i=4, j=4),
-                    in_=src.rearrange("p j a (c i) -> p a c j i", i=4),
-                )
-            else:
-                nc.vector.tensor_copy(
-                    out=dst.rearrange("p a (c i j) -> p a c j i", i=4, j=4),
-                    in_=src.rearrange("p j a (c i) -> p a c j i", i=4),
-                )
-
-        def quant(g, chunks):
-            for (c0, c1) in chunks:
-                nc.vector.quantize_mx(
-                    out=xc[g][:, c0:c1].bitcast(FP8X4), scales=xs[g][:, c0:c1], in_=grp[g][:, 4 * c0:4 * c1]
-                )
-
-        def prepare(pi, g, with_weights):
-            b0 = 2 * pi
-            even_on_scalar = (pi, g) != (1, 0)
-            regroup(b0, g, 1, 0, SPLIT[1], False)
-            regroup(b0, g, 0, 0, SPLIT[0], False)
-            if with_weights:
-                weights_quant(g)
-            regroup(b0, g, 1, SPLIT[1], 16, True)
-            regroup(b0, g, 0, SPLIT[0], 16, even_on_scalar)
-            regroup(b0 + 1, g, 1, 0, SPLIT[1], False)
-            if (pi, g) == (0, 0):
-                quant(g, CHUNKS[pi][0])
-                regroup(b0 + 1, g, 0, 0, SPLIT[0], False)
-            else:
-                regroup(b0 + 1, g, 0, 0, SPLIT[0], False)
-                quant(g, CHUNKS[pi][0])
-            quant(g, CHUNKS[pi][1])
-            regroup(b0 + 1, g, 1, SPLIT[1], 16, True)
-            regroup(b0 + 1, g, 0, SPLIT[0], 16, even_on_scalar)
-            quant(g, CHUNKS[pi][2])
-
-        def one_pass(r, i, m, g, k, col, start, stop):
-            n = 512 if i < 4 else 128
-            s = WIN0[r] + 512 * i + SHIFT[r][k]
-            q = 2 * k + m
-            nc.tensor.matmul_mx(
-                out=ps[:, col:col + n],
-                lhsT=wc[g][:, q * P:(q + 1) * P].bitcast(FP8X4),
-                lhsT_scale=ws[g][:, q * P:(q + 1) * P],
-                rhs=xc[g][:, s:s + n].bitcast(FP8X4),
-                rhs_scale=xs[g][:, s:s + n],
-                start=start,
-                stop=stop,
+            copy_on(
+                eng,
+                dst.rearrange("p a (c i j) -> p a c j i", i=4, j=4),
+                src.rearrange("p j a (c i) -> p a c j i", i=4),
             )
 
-        def drain(r, i, m, col, on_vector):
+        def q(g, c0, c1):
+            nc.vector.quantize_mx(
+                out=xc[g][:, c0:c1].bitcast(FP8X4), scales=xs[g][:, c0:c1], in_=grp[g][:, 4 * c0:4 * c1]
+            )
+
+        def bank_col(r, i, m):
+            return ((6 + (i % 2) * 4 + 2 * m + 1 - r) % 8) * 512
+
+        seen = {}
+
+        def mm(r, i, m, g, k):
             n = 512 if i < 4 else 128
+            s = WIN0[r] + 512 * i + SHIFT[r][k]
+            qq = 2 * k + m
+            c = seen.get((r, i, m), 0)
+            seen[(r, i, m)] = c + 1
+            col = bank_col(r, i, m)
+            nc.tensor.matmul_mx(
+                out=ps[:, col:col + n],
+                lhsT=wc[g][:, qq * P:(qq + 1) * P].bitcast(FP8X4),
+                lhsT_scale=ws[g][:, qq * P:(qq + 1) * P],
+                rhs=xc[g][:, s:s + n].bitcast(FP8X4),
+                rhs_scale=xs[g][:, s:s + n],
+                start=c == 0,
+                stop=c == 5,
+            )
+
+        def dr(r, i, m, eng):
+            n = 512 if i < 4 else 128
+            col = bank_col(r, i, m)
             wst = WIN0[r] + 512 * i
             ov = osb[m][:].rearrange("p (b a r w) -> p b a r w", b=4, a=16, r=2)
             for (pi, s0, ns, w0, w1) in pieces(r, wst, n):
                 j0 = col + FIRST[r] + PAIR * pi + 33 * s0 + w0 - wst
                 dst = ov[:, 2 * pi + s0 % 2, down(15 - s0 // 2, ns), r, w0:w1]
                 src = rows(ps[:], 4096, j0, ns, 66, w1 - w0)
-                if on_vector:
-                    nc.vector.tensor_copy(out=dst, in_=src)
-                else:
-                    nc.scalar.copy(out=dst, in_=src)
+                copy_on(eng, dst, src)
 
-        def store(i, m):
+        def st(i, m):
             for (pi, h0, h1) in STORES[i]:
                 nc.sync.dma_start(
                     out=out[2 * pi:2 * pi + 2, m * P:(m + 1) * P, h0:h1, :].rearrange("b o h w -> o b (h w)"),
                     in_=osb[m][:].rearrange("p (b c) -> p b c", b=4)[:, 2 * pi:2 * pi + 2, 32 * h0:32 * h1],
                 )
 
-        def groups(i0):
-            return [(r, i, m) for i in (i0, i0 + 1) for m in range(2) for r in (1, 0)]
+        def mms(i, g, rks, ms=(0, 1)):
+            for (r, k) in rks:
+                for m in ms:
+                    mm(r, i, m, g, k)
 
-        def bank_of(n):
-            return ((6 + n) % 8) * 512
+        ODD = ((1, 1), (0, 2), (0, 0))
+        QO = {(0, 0): ((2240, 2752), (2752, 2816)), (0, 1): ((2816, 3328),), (1, 0): ((3328, 3840),), (1, 1): ((3840, 4352), (4352, 4480))}
+        QE = {(0, 0): ((0, 64), (64, 576)), (0, 1): ((576, 1088),), (1, 0): ((1088, 1600),), (1, 1): ((1600, 2112), (2112, 2240))}
+        AO = ((0, 10), (10, 16))
+        AE = ((0, 8), (8, 16))
 
-        def sweep(i0, g, ns):
-            for n in ns:
-                (r, i, m) = groups(i0)[n]
-                for k in range(3):
-                    one_pass(r, i, m, g, k, bank_of(n), g == 0 and k == 0, g == 1 and k == 2)
-                if g == 1:
-                    drain(r, i, m, bank_of(n), i0 == 2 and m == 1)
-                    if r == 0:
-                        store(i, m)
+        def qs(g, chunks):
+            for (c0, c1) in chunks:
+                q(g, c0, c1)
 
-        weights_out(0)
-        prepare(0, 0, True)
-        weights_out(1)
-        for (r, k) in ((1, 1), (0, 2), (0, 0), (1, 2), (1, 0), (0, 1)):
+        def rgo(pi, g, h, engs="VV"):
+            for e in range(2):
+                rg(2 * pi + e, g, 1, AO[h][0], AO[h][1], engs[e])
+
+        def rge(pi, g, h, engs="SS"):
+            for e in range(2):
+                rg(2 * pi + e, g, 0, AE[h][0], AE[h][1], engs[e])
+
+        def pe_odd(i, g):
+            mms(i, g, ODD)
+
+        def pe_even(i, g, engs="SS"):
             for m in range(2):
-                one_pass(r, 0, m, 0, k, bank_of(groups(0).index((r, 0, m))), (r, k) in ((1, 1), (0, 2)), False)
-        sweep(0, 0, range(4, 8))
-        prepare(0, 1, True)
-        prepare(1, 0, False)
-        sweep(0, 1, range(8))
-        prepare(1, 1, False)
-        sweep(2, 0, range(8))
-        sweep(2, 1, range(8))
-        for n, (r, m) in enumerate(((1, 0), (0, 0), (1, 1), (0, 1))):
-            for g in range(2):
+                mm(1, i, m, g, 0)
+                mm(1, i, m, g, 2)
+                if g == 1:
+                    dr(1, i, m, engs[m])
+                mm(0, i, m, g, 1)
+                if g == 1:
+                    dr(0, i, m, engs[m])
+                    st(i, m)
+
+        for g in range(2):
+            for m in range(2):
+                load_w(g, m)
+        load_x(0, 0, 16, 32)
+        load_x(1, 0, 16, 32)
+        load_x(0, 0, 0, 16)
+        load_x(1, 0, 0, 16)
+        for (b, g) in ((0, 1), (1, 1), (2, 0), (3, 0), (2, 1), (3, 1)):
+            load_x(b, g)
+        WC = 336
+        W1 = 352
+        for m in range(2):
+            wsrt(0, m, 0, WC, "V")
+            wsrt(0, m, WC, 512, "S")
+        for k in range(3):
+            wtrans(0, k)
+        for m in range(2):
+            wsrt(1, m, 0, W1, "V")
+        for k in range(3):
+            wout(0, k, "S")
+        for m in range(2):
+            wsrt(1, m, W1, 512, "S")
+        for k in range(3):
+            wtrans(1, k)
+        wq(0, 0, 512)
+        rg(0, 0, 1, 0, 8, "V")
+        wq(0, 512, 768)
+        rg(1, 0, 1, 0, 8, "V")
+        q(0, 2240, 2752)
+        mms(0, 0, ((1, 1), (0, 2)))
+        rg(0, 0, 0, 0, 8, "S")
+        rg(1, 0, 0, 0, 8, "V")
+        qs(0, QE[(0, 0)])
+        pe_even(0, 0)
+        for k in range(3):
+            wout(1, k, "S")
+        rg(0, 0, 1, 8, 16, "V")
+        rg(1, 0, 1, 8, 16, "V")
+        rge(0, 0, 1, "SS")
+        qs(0, ((2752, 2816), (2816, 3328)))
+        mms(0, 0, ((0, 0),))
+        pe_odd(1, 0)
+
+        rg(0, 1, 1, 0, 10, "V")
+        qs(0, QE[(0, 1)])
+        pe_even(1, 0)
+        rg(1, 1, 1, 0, 10, "V")
+        rge(0, 1, 0)
+        wq(1, 0, 512)
+        wq(1, 512, 768)
+        qs(1, QO[(0, 0)])
+        pe_odd(0, 1)
+        rgo(0, 1, 1)
+        qs(1, QE[(0, 0)])
+        rge(0, 1, 1)
+        qs(1, QO[(0, 1)])
+        rgo(1, 0, 0)
+        rge(1, 0, 0, "SS")
+        pe_even(0, 1)
+        pe_odd(1, 1)
+        qs(1, QE[(0, 1)])
+        qs(0, QO[(1, 0)])
+        rgo(1, 0, 1)
+        pe_even(1, 1)
+        pe_odd(2, 0)
+        qs(0, QE[(1, 0)])
+        pe_even(2, 0)
+        rge(1, 0, 1, "VV")
+        qs(0, QO[(1, 1)])
+        pe_odd(3, 0)
+        rgo(1, 1, 0)
+        qs(0, QE[(1, 1)])
+        pe_even(3, 0)
+        rge(1, 1, 0)
+        qs(1, QO[(1, 0)])
+        pe_odd(2, 1)
+        rgo(1, 1, 1)
+        qs(1, QE[(1, 0)])
+        rge(1, 1, 1)
+        qs(1, QO[(1, 1)])
+        qs(1, QE[(1, 1)])
+        pe_even(2, 1, "SV")
+        for m in range(2):
+            for r in (1, 0):
                 for k in range(3):
-                    one_pass(r, 4, m, g, k, bank_of(n), g == 0 and k == 0, g == 1 and k == 2)
-            drain(r, 4, m, bank_of(n), m == 1)
-            if r == 0:
-                store(4, m)
+                    mm(r, 3, m, 1, k)
+                dr(r, 3, m, "SV"[r])
+            st(3, m)
+        for m in range(2):
+            for r in (1, 0):
+                for g in range(2):
+                    for k in range(3):
+                        mm(r, 4, m, g, k)
+                dr(r, 4, m, "SV"[r])
+            st(4, m)

@@ -158,11 +158,15 @@ def tile_skeletonconv_t_kernel(tc, x, weight, dilation, step, out):
             base = 4 * (FIRST[r] + PAIR * (b // 2) + 33 * (b % 2) + 66 * a0)
             dst = rows(grp[g], 4 * NCOL, base, a1 - a0, 264, 128)
             src = raw[(b, g)][:].rearrange("p (j a r w) -> p j a r w", j=4, a=16, r=2)[:, :, down(15 - a0, a1 - a0), r, :]
-            copy_on(
-                eng,
-                dst.rearrange("p a (c i j) -> p a c j i", i=4, j=4),
-                src.rearrange("p j a (c i) -> p a c j i", i=4),
-            )
+            if eng == "S":
+                nc.scalar.copy(
+                    out=dst.rearrange("p a (w j) -> p a w j", j=4), in_=src.rearrange("p j a w -> p a w j")
+                )
+            else:
+                nc.vector.tensor_copy(
+                    out=dst.rearrange("p a (c i j) -> p a c j i", i=4, j=4),
+                    in_=src.rearrange("p j a (c i) -> p a c j i", i=4),
+                )
 
         def q(g, c0, c1):
             nc.vector.quantize_mx(

@@ -123,11 +123,16 @@ def tile_skeletonconv_t_kernel(tc, x, weight, dilation, step, out):
             )
 
         def wsrt(g, m, c0, c1, eng):
-            copy_on(
-                eng,
-                wsort[g][:, m * 1536:(m + 1) * 1536].rearrange("o (k c) -> o c k", k=3)[:, c0:c1, :],
-                wraw[g][:, m * 1536:(m + 1) * 1536].rearrange("o (c k) -> o c k", k=3)[:, c0:c1, :],
-            )
+            if eng == "S":
+                nc.scalar.copy(
+                    out=wsort[g][:, m * 1536:(m + 1) * 1536].rearrange("o (k c) -> o k c", k=3)[:, :, c0:c1],
+                    in_=wraw[g][:, m * 1536:(m + 1) * 1536].rearrange("o (c k) -> o k c", k=3)[:, :, c0:c1],
+                )
+            else:
+                nc.vector.tensor_copy(
+                    out=wsort[g][:, m * 1536:(m + 1) * 1536].rearrange("o (k c) -> o c k", k=3)[:, c0:c1, :],
+                    in_=wraw[g][:, m * 1536:(m + 1) * 1536].rearrange("o (c k) -> o c k", k=3)[:, c0:c1, :],
+                )
 
         def wtrans(g, k, ms=(0, 1)):
             wsf = wsort[g][:].bitcast(F32)

@@ -91,6 +91,10 @@ def tile_skeletonconv_t_kernel(tc, x, weight, dilation, step, out):
         ws = [keep.tile([P, 768], U8, name="ws%d" % g, align_bytes=64) for g in range(2)]
         osb = [keep.tile([P, 4096], F32, name="osb%d" % m) for m in range(2)]
 
+        scr = keep.tile([P, 2], F32, name="scr")
+        nc.vector.memset(scr[:, 0:1], 0.0)
+        nc.scalar.copy(out=scr[:, 1:2], in_=scr[:, 0:1])
+
         gf = grp_all[:].bitcast(F32).rearrange("p (g c) -> p g c", g=2)
         for pi in range(2):
             for r in (1, 0):
@@ -142,6 +146,31 @@ def tile_skeletonconv_t_kernel(tc, x, weight, dilation, step, out):
                     nc.tensor.transpose(
                         ps[:, bank * 512 + m * 256 + u * P:bank * 512 + m * 256 + (u + 1) * P],
                         wsf[:, (m * 3 + k) * 256 + u:(m * 3 + k + 1) * 256:2],
+                        ident[:],
+                    )
+
+        def wsrt2(g, m, u, p0, p1, eng):
+            dstw = wsort[g][:, m * 1536:(m + 1) * 1536]
+            srcw = wraw[g][:, m * 1536:(m + 1) * 1536]
+            if eng == "S":
+                nc.scalar.copy(
+                    out=dstw.rearrange("o (k u p e) -> o u k p e", k=3, u=2, e=2)[:, u, :, p0:p1, :],
+                    in_=srcw.rearrange("o (p u e k) -> o u k p e", u=2, e=2, k=3)[:, u, :, p0:p1, :],
+                )
+            else:
+                nc.vector.tensor_copy(
+                    out=dstw.rearrange("o (k u p e) -> o u p e k", k=3, u=2, e=2)[:, u, p0:p1, :, :],
+                    in_=srcw.rearrange("o (p u e k) -> o u p e k", u=2, e=2, k=3)[:, u, p0:p1, :, :],
+                )
+
+        def wtrans2(g, k, ms=(0, 1)):
+            wsf = wsort[g][:].bitcast(F32)
+            bank = 3 * g + k
+            for m in ms:
+                for u in range(2):
+                    nc.tensor.transpose(
+                        ps[:, bank * 512 + m * 256 + u * P:bank * 512 + m * 256 + (u + 1) * P],
+                        wsf[:, (m * 3 + k) * 256 + u * P:(m * 3 + k) * 256 + (u + 1) * P],
                         ident[:],
                     )
 
@@ -264,24 +293,23 @@ def tile_skeletonconv_t_kernel(tc, x, weight, dilation, step, out):
         load_x(1, 0, 0, 16)
         for (b, g) in ((0, 1), (1, 1), (2, 0), (3, 0), (2, 1), (3, 1)):
             load_x(b, g)
-        WC = 336
-        W1 = 352
+        PC = 48
         for m in range(2):
-            wsrt(0, m, 0, WC, "V")
-            wsrt(0, m, WC, 512, "S")
+            wsrt2(0, m, 0, 0, 128, "V")
+            wsrt2(0, m, 1, 0, PC, "V")
+            wsrt2(0, m, 1, PC, 128, "S")
         for k in range(3):
-            wtrans(0, k)
+            wtrans2(0, k)
         for m in range(2):
-            wsrt(1, m, 0, W1, "V")
+            for u in range(2):
+                wsrt2(1, m, u, 0, 128, "V")
         for k in range(3):
             wout(0, k, "S")
-        for m in range(2):
-            wsrt(1, m, W1, 512, "S")
         for k in range(3):
-            wtrans(1, k)
+            wtrans2(1, k)
         wq(0, 0, 512)
-        rg(0, 0, 1, 0, 8, "V")
         wq(0, 512, 768)
+        rg(0, 0, 1, 0, 8, "S")
         rg(1, 0, 1, 0, 8, "V")
         q(0, 2240, 2752)
         mms(0, 0, ((1, 1), (0, 2)))
@@ -299,11 +327,11 @@ def tile_skeletonconv_t_kernel(tc, x, weight, dilation, step, out):
         pe_odd(1, 0)
 
         rg(0, 1, 1, 0, 10, "V")
+        wq(1, 0, 512)
         qs(0, QE[(0, 1)])
         pe_even(1, 0)
         rg(1, 1, 1, 0, 10, "V")
         rge(0, 1, 0)
-        wq(1, 0, 512)
         wq(1, 512, 768)
         qs(1, QO[(0, 0)])
         pe_odd(0, 1)

@@ -95,6 +95,13 @@ def tile_skeletonconv_t_kernel(tc, x, weight, dilation, step, out):
         nc.vector.memset(scr[:, 0:1], 0.0)
         nc.scalar.copy(out=scr[:, 1:2], in_=scr[:, 0:1])
 
+        warm = keep.tile([P, 512], BF16, name="warm")
+        nc.vector.memset(warm[:], 0.0)
+
+        def idle(n):
+            for t in range(n):
+                nc.tensor.matmul(ps[:, 6 * 512:7 * 512], lhsT=warm[:, 0:P], rhs=warm[:], start=True, stop=True)
+
         gf = grp_all[:].bitcast(F32).rearrange("p (g c) -> p g c", g=2)
         for pi in range(2):
             for r in (1, 0):
@@ -119,10 +126,10 @@ def tile_skeletonconv_t_kernel(tc, x, weight, dilation, step, out):
             )
 
         def load_x(b, g, h0=0, h1=32):
-            if (b, g) not in raw:
-                raw[(b, g)] = rawp.tile([P, 4096], BF16, name="raw")
+            t = rawp.tile([P, 4096], BF16, name="raw")
+            raw.setdefault((b, g), []).append((h0, h1, t))
             nc.sync.dma_start(
-                out=raw[(b, g)][:].rearrange("p (j c) -> p j c", j=4)[:, :, 32 * h0:32 * h1],
+                out=t[:, 0:128 * (h1 - h0)].rearrange("p (j c) -> p j c", j=4),
                 in_=x[b, g * 512:(g + 1) * 512, h0:h1, :].rearrange("(p j) h w -> p j (h w)", j=4),
             )
 
@@ -191,7 +198,10 @@ def tile_skeletonconv_t_kernel(tc, x, weight, dilation, step, out):
         def rg(b, g, r, a0, a1, eng):
             base = 4 * (FIRST[r] + PAIR * (b // 2) + 33 * (b % 2) + 66 * a0)
             dst = rows(grp[g], 4 * NCOL, base, a1 - a0, 264, 128)
-            src = raw[(b, g)][:].rearrange("p (j a r w) -> p j a r w", j=4, a=16, r=2)[:, :, down(15 - a0, a1 - a0), r, :]
+            (h0, h1, t) = [e for e in raw[(b, g)] if e[0] <= 2 * (16 - a1) and 2 * (16 - a0) <= e[1]][0]
+            src = t[:, 0:128 * (h1 - h0)].rearrange("p (j a r w) -> p j a r w", j=4, r=2, w=32)[
+                :, :, down(15 - a0 - h0 // 2, a1 - a0), r, :
+            ]
             if eng == "S":
                 nc.scalar.copy(
                     out=dst.rearrange("p a (w j) -> p a w j", j=4), in_=src.rearrange("p j a w -> p a w j")
@@ -294,12 +304,14 @@ def tile_skeletonconv_t_kernel(tc, x, weight, dilation, step, out):
         for (b, g) in ((0, 1), (1, 1), (2, 0), (3, 0), (2, 1), (3, 1)):
             load_x(b, g)
         PC = 48
+        idle(8)
         for m in range(2):
             wsrt2(0, m, 0, 0, 128, "V")
             wsrt2(0, m, 1, 0, PC, "V")
             wsrt2(0, m, 1, PC, 128, "S")
         for k in range(3):
             wtrans2(0, k)
+        idle(2)
         for m in range(2):
             for u in range(2):
                 wsrt2(1, m, u, 0, 128, "V")
@@ -307,14 +319,15 @@ def tile_skeletonconv_t_kernel(tc, x, weight, dilation, step, out):
             wout(0, k, "S")
         for k in range(3):
             wtrans2(1, k)
+        idle(3)
         wq(0, 0, 512)
+        rg(0, 0, 1, 0, 8, "V")
         wq(0, 512, 768)
-        rg(0, 0, 1, 0, 8, "S")
         rg(1, 0, 1, 0, 8, "V")
         q(0, 2240, 2752)
         mms(0, 0, ((1, 1), (0, 2)))
         rg(0, 0, 0, 0, 8, "S")
-        rg(1, 0, 0, 0, 8, "V")
+        rg(1, 0, 0, 0, 8, "S")
         qs(0, QE[(0, 0)])
         pe_even(0, 0)
         for k in range(3):
@@ -369,12 +382,12 @@ def tile_skeletonconv_t_kernel(tc, x, weight, dilation, step, out):
             for r in (1, 0):
                 for k in range(3):
                     mm(r, 3, m, 1, k)
-                dr(r, 3, m, "SV"[r])
+                dr(r, 3, m, "SV"[m])
             st(3, m)
         for m in range(2):
             for r in (1, 0):
                 for g in range(2):
                     for k in range(3):
                         mm(r, 4, m, g, k)
-                dr(r, 4, m, "SV"[r])
+                dr(r, 4, m, "SV"[m])
             st(4, m)

@@ -8,64 +8,29 @@ from concourse.masks import make_identity
 FP8X4 = mybir.dt.float8_e4m3fn_x4
 BF16 = mybir.dt.bfloat16
 F32 = mybir.dt.float32
+I32 = mybir.dt.int32
 U32 = mybir.dt.uint32
 U8 = mybir.dt.uint8
 
 FLOPS = 2 * 4 * 1024 * 1024 * 256 * 3
 
 P = 128
-NCOL = 4480
-FIRST = (65, 2240)
-WIN0 = (64, 2240)
-PAIR = 1120
-SHIFT = ((2240, 0, 2176), (-2176, 0, -2240))
-STORES = {0: ((0, 18, 32),), 1: ((0, 2, 18),), 2: ((0, 0, 2), (1, 20, 32)), 3: ((1, 4, 20),), 4: ((1, 0, 4),)}
-
-
-def rows(ap2d, total, start, n, pitch, width):
-    if n == 1:
-        return ap2d[:, start:start + width].rearrange("p (a c) -> p a c", a=1)
-    if start + n * pitch <= total:
-        return ap2d[:, start:start + n * pitch].rearrange("p (a c) -> p a c", c=pitch)[:, :, 0:width]
-    lead = pitch - width
-    return ap2d[:, start - lead:start - lead + n * pitch].rearrange("p (a c) -> p a c", c=pitch)[:, :, lead:pitch]
+NCOL = 4544
+FIRST = (65, 2304)
+PAIR = 1152
+WIN0 = (64, 2304)
+WINDOWS = {(i, m): (i // 2, 512 * (i % 2), 512) for i in range(4) for m in range(2)}
+WINDOWS[(3, 1)] = (1, 512, 256)
+WINDOWS[(4, 1)] = (1, 768, 256)
+STORES = {(i, m): ((18, 32), (2, 18))[i % 2] for i in range(4) for m in range(2)}
+STORES[(3, 1)] = (10, 18)
+STORES[(4, 1)] = (2, 10)
+SHIFT = ((2304, 0, 2240), (-2240, 0, -2304))
 
 
 def down(first, n):
     last = first - n
     return slice(first, last if last >= 0 else None, -1)
-
-
-def pieces(r, wst, n):
-    res = []
-    for pi in range(2):
-        base = FIRST[r] + PAIR * pi
-        lo = max(wst - base, 0)
-        hi = min(wst + n - base, 1056)
-        if lo >= hi:
-            continue
-        full = []
-        for s in range(lo // 33, (hi - 1) // 33 + 1):
-            w0 = max(lo - 33 * s, 0)
-            w1 = min(hi - 33 * s, 32)
-            if w1 <= w0:
-                continue
-            if w0 == 0 and w1 == 32:
-                full.append(s)
-            else:
-                res.append((pi, s, 1, w0, w1))
-        for b2 in range(2):
-            ss = [s for s in full if s % 2 == b2]
-            if ss:
-                res.append((pi, ss[0], len(ss), 0, 32))
-    return res
-
-
-CHUNKS = {
-    0: (((2240, 2752), (2752, 2816)), ((0, 64), (64, 576)), ((2816, 3328), (576, 1088))),
-    1: (((3328, 3840),), ((1088, 1600),), ((3840, 4352), (1600, 2112), (4352, 4480), (2112, 2240))),
-}
-SPLIT = (8, 10)
 
 
 def tile_skeletonconv_t_kernel(tc, x, weight, dilation, step, out):
@@ -85,6 +50,8 @@ def tile_skeletonconv_t_kernel(tc, x, weight, dilation, step, out):
         grp = [grp_all[:, g * 4 * NCOL:(g + 1) * 4 * NCOL] for g in range(2)]
         xc = [keep.tile([P, NCOL], U32, name="xc%d" % g, align_bytes=64) for g in range(2)]
         xs = [keep.tile([P, NCOL], U8, name="xs%d" % g, align_bytes=64) for g in range(2)]
+        lc = [keep.tile([P, 384], U32, name="lc%d" % g, align_bytes=64) for g in range(2)]
+        ls = [keep.tile([P, 384], U8, name="ls%d" % g, align_bytes=64) for g in range(2)]
         wsort = [keep.tile([P, 3072], BF16, name="wsort%d" % g) for g in range(2)]
         wgrp = [keep.tile([P, 3072], BF16, name="wgrp%d" % g, align_bytes=64) for g in range(2)]
         wc = [keep.tile([P, 768], U32, name="wc%d" % g, align_bytes=64) for g in range(2)]
@@ -95,22 +62,30 @@ def tile_skeletonconv_t_kernel(tc, x, weight, dilation, step, out):
         nc.vector.memset(scr[:, 0:1], 0.0)
         nc.scalar.copy(out=scr[:, 1:2], in_=scr[:, 0:1])
 
-        warm = keep.tile([P, 512], BF16, name="warm")
-        nc.vector.memset(warm[:], 0.0)
+        warm = osb[1][:, 0:256].bitcast(BF16)
+        nc.vector.memset(osb[1][:, 0:256], 0.0)
 
         def idle(n):
             for t in range(n):
-                nc.tensor.matmul(ps[:, 6 * 512:7 * 512], lhsT=warm[:, 0:P], rhs=warm[:], start=True, stop=True)
+                nc.tensor.matmul(ps[:, 6 * 512:7 * 512], lhsT=warm[:, 0:P], rhs=warm, start=True, stop=True)
 
         gf = grp_all[:].bitcast(F32).rearrange("p (g c) -> p g c", g=2)
         for pi in range(2):
             for r in (1, 0):
                 lo = 2 * (FIRST[r] + PAIR * pi + 32)
                 nc.vector.memset(gf[:, :, lo:lo + 32 * 66].rearrange("p g (a c) -> p g a c", c=66)[:, :, :, 0:2], 0.0)
-        for (c0, c1) in ((0, 65), (1121, 1185), (3296, 3360), (4416, 4480)):
-            nc.vector.memset(gf[:, :, 2 * c0:2 * c1], 0.0)
+        for c in (64, 1216):
+            nc.vector.memset(gf[:, :, 2 * c:2 * c + 2], 0.0)
+        for g in range(2):
+            for (c0, w) in ((0, 64), (3360, 32)):
+                nc.vector.memset(xc[g][:, c0:c0 + 1152 + w].bitcast(I32)[:, 0:w], 0)
+                nc.vector.memset(xc[g][:, c0 + 1152:c0 + 1152 + w].bitcast(I32), 0)
+                nc.vector.memset(xs[g][:, c0:c0 + w].bitcast(I32), 0)
+                nc.vector.memset(xs[g][:, c0 + 1152:c0 + 1152 + w].bitcast(I32), 0)
+            nc.vector.memset(lc[g][:, 0:64].bitcast(I32), 0)
+            nc.vector.memset(ls[g][:, 0:64].bitcast(I32), 0)
 
-        wraw = [rawp.tile([P, 4096], BF16, name="raw") for g in range(2)]
+        wraw = {}
         raw = {}
 
         def copy_on(eng, out, in_):
@@ -120,8 +95,12 @@ def tile_skeletonconv_t_kernel(tc, x, weight, dilation, step, out):
                 nc.vector.tensor_copy(out=out, in_=in_)
 
         def load_w(g, m):
+            t = wraw.get(g)
+            if t is None:
+                t = rawp.tile([P, 4096], BF16, name="raw")
+                wraw[g] = t
             nc.sync.dma_start(
-                out=wraw[g][:, m * 1536:(m + 1) * 1536],
+                out=t[:, m * 1536:(m + 1) * 1536],
                 in_=weight[m * P:(m + 1) * P, g * 512:(g + 1) * 512, :].rearrange("o c k -> o (c k)"),
             )
 
@@ -133,30 +112,7 @@ def tile_skeletonconv_t_kernel(tc, x, weight, dilation, step, out):
                 in_=x[b, g * 512:(g + 1) * 512, h0:h1, :].rearrange("(p j) h w -> p j (h w)", j=4),
             )
 
-        def wsrt(g, m, c0, c1, eng):
-            if eng == "S":
-                nc.scalar.copy(
-                    out=wsort[g][:, m * 1536:(m + 1) * 1536].rearrange("o (k c) -> o k c", k=3)[:, :, c0:c1],
-                    in_=wraw[g][:, m * 1536:(m + 1) * 1536].rearrange("o (c k) -> o k c", k=3)[:, :, c0:c1],
-                )
-            else:
-                nc.vector.tensor_copy(
-                    out=wsort[g][:, m * 1536:(m + 1) * 1536].rearrange("o (k c) -> o c k", k=3)[:, c0:c1, :],
-                    in_=wraw[g][:, m * 1536:(m + 1) * 1536].rearrange("o (c k) -> o c k", k=3)[:, c0:c1, :],
-                )
-
-        def wtrans(g, k, ms=(0, 1)):
-            wsf = wsort[g][:].bitcast(F32)
-            bank = 3 * g + k
-            for m in ms:
-                for u in range(2):
-                    nc.tensor.transpose(
-                        ps[:, bank * 512 + m * 256 + u * P:bank * 512 + m * 256 + (u + 1) * P],
-                        wsf[:, (m * 3 + k) * 256 + u:(m * 3 + k + 1) * 256:2],
-                        ident[:],
-                    )
-
-        def wsrt2(g, m, u, p0, p1, eng):
+        def wsrt(g, m, u, p0, p1, eng):
             dstw = wsort[g][:, m * 1536:(m + 1) * 1536]
             srcw = wraw[g][:, m * 1536:(m + 1) * 1536]
             if eng == "S":
@@ -170,10 +126,10 @@ def tile_skeletonconv_t_kernel(tc, x, weight, dilation, step, out):
                     in_=srcw.rearrange("o (p u e k) -> o u p e k", u=2, e=2, k=3)[:, u, p0:p1, :, :],
                 )
 
-        def wtrans2(g, k, ms=(0, 1)):
+        def wtrans(g, k):
             wsf = wsort[g][:].bitcast(F32)
             bank = 3 * g + k
-            for m in ms:
+            for m in range(2):
                 for u in range(2):
                     nc.tensor.transpose(
                         ps[:, bank * 512 + m * 256 + u * P:bank * 512 + m * 256 + (u + 1) * P],
@@ -197,10 +153,14 @@ def tile_skeletonconv_t_kernel(tc, x, weight, dilation, step, out):
 
         def rg(b, g, r, a0, a1, eng):
             base = 4 * (FIRST[r] + PAIR * (b // 2) + 33 * (b % 2) + 66 * a0)
-            dst = rows(grp[g], 4 * NCOL, base, a1 - a0, 264, 128)
+            n = a1 - a0
+            if b % 2 == 0 or a1 < 16:
+                dst = grp[g][:, base:base + 264 * n].rearrange("p (a c) -> p a c", c=264)[:, :, 0:128]
+            else:
+                dst = grp[g][:, base - 132:base - 132 + 264 * n].rearrange("p (a c) -> p a c", c=264)[:, :, 132:260]
             (h0, h1, t) = [e for e in raw[(b, g)] if e[0] <= 2 * (16 - a1) and 2 * (16 - a0) <= e[1]][0]
             src = t[:, 0:128 * (h1 - h0)].rearrange("p (j a r w) -> p j a r w", j=4, r=2, w=32)[
-                :, :, down(15 - a0 - h0 // 2, a1 - a0), r, :
+                :, :, down(15 - a0 - h0 // 2, n), r, :
             ]
             if eng == "S":
                 nc.scalar.copy(
@@ -223,8 +183,8 @@ def tile_skeletonconv_t_kernel(tc, x, weight, dilation, step, out):
         seen = {}
 
         def mm(r, i, m, g, k):
-            n = 512 if i < 4 else 128
-            s = WIN0[r] + 512 * i + SHIFT[r][k]
+            (pi, off, n) = WINDOWS[(i, m)]
+            s = WIN0[r] + PAIR * pi + off + SHIFT[r][k]
             qq = 2 * k + m
             c = seen.get((r, i, m), 0)
             seen[(r, i, m)] = c + 1
@@ -239,155 +199,253 @@ def tile_skeletonconv_t_kernel(tc, x, weight, dilation, step, out):
                 stop=c == 5,
             )
 
+        def mml(m, g, k, c):
+            col = bank_col(1, 5, m)
+            qq = 2 * k + m
+            nc.tensor.matmul_mx(
+                out=ps[:, col:col + P],
+                lhsT=wc[g][:, qq * P:(qq + 1) * P].bitcast(FP8X4),
+                lhsT_scale=ws[g][:, qq * P:(qq + 1) * P],
+                rhs=lc[g][:, k * P:(k + 1) * P].bitcast(FP8X4),
+                rhs_scale=ls[g][:, k * P:(k + 1) * P],
+                start=c == 0,
+                stop=c == 5,
+            )
+
         def dr(r, i, m, eng):
-            n = 512 if i < 4 else 128
-            col = bank_col(r, i, m)
-            wst = WIN0[r] + 512 * i
+            (pi, off, n) = WINDOWS[(i, m)]
             ov = osb[m][:].rearrange("p (b a r w) -> p b a r w", b=4, a=16, r=2)
-            for (pi, s0, ns, w0, w1) in pieces(r, wst, n):
-                j0 = col + FIRST[r] + PAIR * pi + 33 * s0 + w0 - wst
-                dst = ov[:, 2 * pi + s0 % 2, down(15 - s0 // 2, ns), r, w0:w1]
-                src = rows(ps[:], 4096, j0, ns, 66, w1 - w0)
-                copy_on(eng, dst, src)
+            lo = off + WIN0[r] - FIRST[r]
+            j0 = bank_col(r, i, m) - lo
+
+            def part(s, w0, w1):
+                if w0 < w1:
+                    copy_on(
+                        eng,
+                        ov[:, 2 * pi + s % 2, 15 - s // 2, r, w0:w1],
+                        ps[:, j0 + 33 * s + w0:j0 + 33 * s + w1],
+                    )
+
+            first = max(lo, 0) // 33
+            if lo > 33 * first:
+                part(first, lo - 33 * first, 32)
+                first += 1
+            last = (lo + n - 32) // 33 + 1
+            a0, a1 = (first + 1) // 2, last // 2
+            if first % 2:
+                part(first, 0, 32)
+            copy_on(
+                eng,
+                ov[:, 2 * pi:2 * pi + 2, down(15 - a0, a1 - a0), r, :],
+                ps[:, j0 + 66 * a0:j0 + 66 * a1].rearrange("p (a e c) -> p e a c", e=2, c=33)[:, :, :, 0:32],
+            )
+            if last % 2:
+                part(last - 1, 0, 32)
+            if last < 31:
+                part(last, 0, lo + n - 33 * last)
+
+        def drl(m, eng):
+            col = bank_col(1, 5, m)
+            ov = osb[m][:].rearrange("p (b h w) -> p b h w", b=4, w=32)
+            copy_on(
+                eng,
+                ov[:, 1:4:2, 0:2, :],
+                ps[:, col:col + P].rearrange("p (h b w) -> p b h w", h=2, b=2),
+            )
+
+        def store(m, b0, b1, h0, h1):
+            nc.sync.dma_start(
+                out=out[b0:b1, m * P:(m + 1) * P, h0:h1, :].rearrange("b o h w -> o b (h w)"),
+                in_=osb[m][:].rearrange("p (b c) -> p b c", b=4)[:, b0:b1, 32 * h0:32 * h1],
+            )
 
         def st(i, m):
-            for (pi, h0, h1) in STORES[i]:
-                nc.sync.dma_start(
-                    out=out[2 * pi:2 * pi + 2, m * P:(m + 1) * P, h0:h1, :].rearrange("b o h w -> o b (h w)"),
-                    in_=osb[m][:].rearrange("p (b c) -> p b c", b=4)[:, 2 * pi:2 * pi + 2, 32 * h0:32 * h1],
+            pi = WINDOWS[(i, m)][0]
+            store(m, 2 * pi, 2 * pi + 2, *STORES[(i, m)])
+
+        def left(g):
+            for (d, c0, lead) in ((64, 1087, 0), (128, 1088, 0), (192, 3327, 1120), (256, 3328, 1120), (320, 1023, 0)):
+                s0 = c0 - lead
+                nc.vector.tensor_copy(
+                    out=lc[g][:, d:d + 64].bitcast(I32).rearrange("p (b w) -> p b w", b=2),
+                    in_=xc[g][:, s0:s0 + 2304].bitcast(I32).rearrange("p (b c) -> p b c", b=2)[:, :, lead:lead + 32],
+                )
+                nc.vector.tensor_copy(
+                    out=ls[g][:, d:d + 64].rearrange("p (b w) -> p b w", b=2),
+                    in_=xs[g][:, s0:s0 + 2304].rearrange("p (b c) -> p b c", b=2)[:, :, lead:lead + 32],
                 )
 
-        def mms(i, g, rks, ms=(0, 1)):
+        QO = {(pi, hh): (2304 + PAIR * pi + 512 * hh, 2816 + PAIR * pi + 512 * hh) for pi in range(2) for hh in range(2)}
+        QE = {(pi, hh): (64 + PAIR * pi + 512 * hh, 576 + PAIR * pi + 512 * hh) for pi in range(2) for hh in range(2)}
+        ODD = ((1, 1), (0, 2), (0, 0))
+
+        def qo(pi, g, hh):
+            q(g, *QO[(pi, hh)])
+            if hh:
+                q(g, QO[(pi, hh)][1], QO[(pi, hh)][1] + 32)
+
+        def qe(pi, g, hh):
+            q(g, *QE[(pi, hh)])
+            if hh:
+                q(g, QE[(pi, hh)][1], QE[(pi, hh)][1] + 32)
+
+        def rgo(pi, g, h, engs="VV"):
+            for e in range(2):
+                rg(2 * pi + e, g, 1, *AO[h], engs[e])
+
+        def rge(pi, g, h, engs="SS"):
+            for e in range(2):
+                rg(2 * pi + e, g, 0, *AE[h], engs[e])
+
+        AO = ((0, 8), (8, 16))
+        AE = ((0, 8), (8, 16))
+
+        def pe(i, g, rks, ms=(0, 1)):
             for (r, k) in rks:
                 for m in ms:
                     mm(r, i, m, g, k)
 
-        ODD = ((1, 1), (0, 2), (0, 0))
-        QO = {(0, 0): ((2240, 2752), (2752, 2816)), (0, 1): ((2816, 3328),), (1, 0): ((3328, 3840),), (1, 1): ((3840, 4352), (4352, 4480))}
-        QE = {(0, 0): ((0, 64), (64, 576)), (0, 1): ((576, 1088),), (1, 0): ((1088, 1600),), (1, 1): ((1600, 2112), (2112, 2240))}
-        AO = ((0, 10), (10, 16))
-        AE = ((0, 8), (8, 16))
+        A = ((1, 1), (0, 2))
+        C = ((0, 0),)
 
-        def qs(g, chunks):
-            for (c0, c1) in chunks:
-                q(g, c0, c1)
+        def pe_b(i, g):
+            pe(i, g, ((1, 0), (1, 2)), (0,))
+            pe(i, g, ((1, 0), (1, 2)), (1,))
+            pe(i, g, ((0, 1),))
 
-        def rgo(pi, g, h, engs="VV"):
-            for e in range(2):
-                rg(2 * pi + e, g, 1, AO[h][0], AO[h][1], engs[e])
-
-        def rge(pi, g, h, engs="SS"):
-            for e in range(2):
-                rg(2 * pi + e, g, 0, AE[h][0], AE[h][1], engs[e])
-
-        def pe_odd(i, g):
-            mms(i, g, ODD)
-
-        def pe_even(i, g, engs="SS"):
-            for m in range(2):
-                mm(1, i, m, g, 0)
-                mm(1, i, m, g, 2)
-                if g == 1:
-                    dr(1, i, m, engs[m])
-                mm(0, i, m, g, 1)
-                if g == 1:
-                    dr(0, i, m, engs[m])
-                    st(i, m)
-
-        for g in range(2):
-            for m in range(2):
-                load_w(g, m)
+        load_w(0, 0)
+        load_w(0, 1)
         load_x(0, 0, 16, 32)
         load_x(1, 0, 16, 32)
+        load_w(1, 0)
+        load_w(1, 1)
         load_x(0, 0, 0, 16)
         load_x(1, 0, 0, 16)
-        for (b, g) in ((0, 1), (1, 1), (2, 0), (3, 0), (2, 1), (3, 1)):
+        for (h0, h1) in ((16, 32), (0, 16)):
+            for b in range(2):
+                load_x(b, 1, h0, h1)
+        for (b, g) in ((2, 0), (3, 0), (2, 1), (3, 1)):
             load_x(b, g)
+        idle(7)
         PC = 48
-        idle(8)
         for m in range(2):
-            wsrt2(0, m, 0, 0, 128, "V")
-            wsrt2(0, m, 1, 0, PC, "V")
-            wsrt2(0, m, 1, PC, 128, "S")
-        for k in range(3):
-            wtrans2(0, k)
-        idle(2)
+            wsrt(0, m, 0, 0, 128, "V")
+            wsrt(0, m, 1, 0, PC, "V")
+            wsrt(0, m, 1, PC, 128, "S")
+        for k in (1, 2, 0):
+            wtrans(0, k)
+        rg(0, 0, 1, 0, 8, "V")
+        wout(0, 1, "S")
+        wout(0, 2, "S")
+        wq(0, 256, 512)
+        rg(1, 0, 1, 0, 8, "V")
+        wq(0, 512, 768)
+        qo(0, 0, 0)
+        wout(0, 0, "S")
+        rge(0, 0, 0)
+        idle(5)
+        pe(0, 0, A)
         for m in range(2):
             for u in range(2):
-                wsrt2(1, m, u, 0, 128, "V")
+                wsrt(1, m, u, 0, 128, "V")
         for k in range(3):
-            wout(0, k, "S")
-        for k in range(3):
-            wtrans2(1, k)
-        idle(3)
-        wq(0, 0, 512)
-        rg(0, 0, 1, 0, 8, "V")
-        wq(0, 512, 768)
-        rg(1, 0, 1, 0, 8, "V")
-        q(0, 2240, 2752)
-        mms(0, 0, ((1, 1), (0, 2)))
-        rg(0, 0, 0, 0, 8, "S")
-        rg(1, 0, 0, 0, 8, "S")
-        qs(0, QE[(0, 0)])
-        pe_even(0, 0)
-        for k in range(3):
-            wout(1, k, "S")
+            wtrans(1, k)
         rg(0, 0, 1, 8, 16, "V")
+        wq(0, 0, 256)
+        qe(0, 0, 0)
+        pe_b(0, 0)
+        rg(0, 0, 0, 8, 16, "S")
         rg(1, 0, 1, 8, 16, "V")
-        rge(0, 0, 1, "SS")
-        qs(0, ((2752, 2816), (2816, 3328)))
-        mms(0, 0, ((0, 0),))
-        pe_odd(1, 0)
-
-        rg(0, 1, 1, 0, 10, "V")
-        wq(1, 0, 512)
-        qs(0, QE[(0, 1)])
-        pe_even(1, 0)
-        rg(1, 1, 1, 0, 10, "V")
+        wout(1, 1, "S")
+        wout(1, 0, "S")
+        wout(1, 2, "S")
+        rg(1, 0, 0, 8, 16, "S")
+        qo(0, 0, 1)
+        pe(0, 0, C)
+        pe(1, 0, A)
+        pe(1, 0, C)
+        rg(0, 1, 1, 0, 8, "V")
+        wq(1, 256, 512)
+        qe(0, 0, 1)
+        pe_b(1, 0)
         rge(0, 1, 0)
+        rg(0, 1, 1, 8, 16, "V")
+        rg(1, 1, 1, 0, 8, "V")
         wq(1, 512, 768)
-        qs(1, QO[(0, 0)])
-        pe_odd(0, 1)
-        rgo(0, 1, 1)
-        qs(1, QE[(0, 0)])
+        qo(0, 1, 0)
+        wq(1, 0, 256)
+        pe(0, 1, A)
+        qe(0, 1, 0)
+        rg(1, 1, 1, 8, 16, "V")
         rge(0, 1, 1)
-        qs(1, QO[(0, 1)])
-        rgo(1, 0, 0)
-        rge(1, 0, 0, "SS")
-        pe_even(0, 1)
-        pe_odd(1, 1)
-        qs(1, QE[(0, 1)])
-        qs(0, QO[(1, 0)])
-        rgo(1, 0, 1)
-        pe_even(1, 1)
-        pe_odd(2, 0)
-        qs(0, QE[(1, 0)])
-        pe_even(2, 0)
-        rge(1, 0, 1, "VV")
-        qs(0, QO[(1, 1)])
-        pe_odd(3, 0)
-        rgo(1, 1, 0)
-        qs(0, QE[(1, 1)])
-        pe_even(3, 0)
+        pe_b(0, 1)
+        qo(0, 1, 1)
+        pe(0, 1, C)
+        pe(1, 1, A)
+        pe(1, 1, C)
+        rge(1, 0, 0)
+        rg(2, 0, 1, 0, 8, "V")
+        qe(0, 1, 1)
+        dr(1, 0, 0, "S")
+        dr(1, 0, 1, "S")
+        pe_b(1, 1)
+        rg(3, 0, 1, 0, 8, "V")
+        dr(0, 0, 0, "S")
+        st(0, 0)
+        dr(0, 0, 1, "S")
+        st(0, 1)
+        rg(2, 0, 1, 8, 16, "V")
+        qo(1, 0, 0)
+        dr(1, 1, 0, "S")
+        dr(1, 1, 1, "S")
+        rg(3, 0, 1, 8, 16, "V")
+        dr(0, 1, 0, "S")
+        st(1, 0)
+        pe(2, 0, A)
+        qe(1, 0, 0)
+        dr(0, 1, 1, "V")
+        st(1, 1)
+        rge(1, 0, 1, "VS")
+        pe_b(2, 0)
+        qo(1, 0, 1)
+        pe(2, 0, C)
+        pe(3, 0, A)
+        pe(3, 0, C)
+        rg(2, 1, 1, 0, 8, "V")
+        qe(1, 0, 1)
         rge(1, 1, 0)
-        qs(1, QO[(1, 0)])
-        pe_odd(2, 1)
-        rgo(1, 1, 1)
-        qs(1, QE[(1, 0)])
+        pe_b(3, 0)
+        rg(3, 1, 1, 0, 8, "V")
+        rg(2, 1, 1, 8, 16, "V")
+        qo(1, 1, 0)
+        pe(2, 1, A)
+        rg(3, 1, 1, 8, 16, "V")
+        qe(1, 1, 0)
         rge(1, 1, 1)
-        qs(1, QO[(1, 1)])
-        qs(1, QE[(1, 1)])
-        pe_even(2, 1, "SV")
-        for m in range(2):
+        qo(1, 1, 1)
+        pe_b(2, 1)
+        qe(1, 1, 1)
+        dr(1, 2, 0, "S")
+        dr(1, 2, 1, "V")
+        pe(2, 1, C)
+        dr(0, 2, 0, "S")
+        st(2, 0)
+        dr(0, 2, 1, "V")
+        st(2, 1)
+        left(0)
+        left(1)
+        for (i, m) in ((3, 0), (3, 1), (4, 1)):
             for r in (1, 0):
+                for g in range(2) if i == 4 else (1,):
+                    for k in (1, 0, 2):
+                        mm(r, i, m, g, k)
+                dr(r, i, m, "SV"[m])
+            st(i, m)
+        for m in range(2):
+            c = 0
+            for g in range(2):
                 for k in range(3):
-                    mm(r, 3, m, 1, k)
-                dr(r, 3, m, "SV"[m])
-            st(3, m)
-        for m in range(2):
-            for r in (1, 0):
-                for g in range(2):
-                    for k in range(3):
-                        mm(r, 4, m, g, k)
-                dr(r, 4, m, "SV"[m])
-            st(4, m)
+                    mml(m, g, k, c)
+                    c += 1
+            drl(m, "SV"[m])
+            store(m, 0, 4, 0, 2)

@@ -321,10 +321,7 @@ def tile_skeletonconv_t_kernel(tc, x, weight, dilation, step, out):
         load_w(1, 1)
         load_x(0, 0, 0, 16)
         load_x(1, 0, 0, 16)
-        for (h0, h1) in ((16, 32), (0, 16)):
-            for b in range(2):
-                load_x(b, 1, h0, h1)
-        for (b, g) in ((2, 0), (3, 0), (2, 1), (3, 1)):
+        for (b, g) in ((0, 1), (1, 1), (2, 0), (3, 0), (2, 1), (3, 1)):
             load_x(b, g)
         idle(7)
         PC = 48

@@ -16,6 +16,8 @@ FLOPS = 2 * 4 * 1024 * 1024 * 256 * 3
 
 P = 128
 NCOL = 4544
+XP = 4608
+XS = 4544
 FIRST = (65, 2304)
 PAIR = 1152
 WIN0 = (64, 2304)
@@ -48,15 +50,19 @@ def tile_skeletonconv_t_kernel(tc, x, weight, dilation, step, out):
 
         grp_all = keep.tile([P, 2 * 4 * NCOL], BF16, name="grp_all", align_bytes=64)
         grp = [grp_all[:, g * 4 * NCOL:(g + 1) * 4 * NCOL] for g in range(2)]
-        xc = [keep.tile([P, NCOL], U32, name="xc%d" % g, align_bytes=64) for g in range(2)]
-        xs = [keep.tile([P, NCOL], U8, name="xs%d" % g, align_bytes=64) for g in range(2)]
-        lc = [keep.tile([P, 384], U32, name="lc%d" % g, align_bytes=64) for g in range(2)]
-        ls = [keep.tile([P, 384], U8, name="ls%d" % g, align_bytes=64) for g in range(2)]
-        wsort = [keep.tile([P, 3072], BF16, name="wsort%d" % g) for g in range(2)]
+        xc_all = keep.tile([P, 2 * XP], U32, name="xc_all", align_bytes=256)
+        xs_all = keep.tile([P, 2 * XS + 0], U8, name="xs_all", align_bytes=256)
+        xc = [xc_all[:, g * XP:g * XP + NCOL] for g in range(2)]
+        xs = [xs_all[:, 0 + g * XS:0 + g * XS + NCOL] for g in range(2)]
+        lc_all = keep.tile([P, 2 * 384], U32, name="lc_all", align_bytes=256)
+        ls_all = keep.tile([P, 2 * 384], U8, name="ls_all", align_bytes=256)
+        lc = [lc_all[:, g * 384:(g + 1) * 384] for g in range(2)]
+        ls = [ls_all[:, g * 384:(g + 1) * 384] for g in range(2)]
         wgrp = [keep.tile([P, 3072], BF16, name="wgrp%d" % g, align_bytes=64) for g in range(2)]
-        wc = [keep.tile([P, 768], U32, name="wc%d" % g, align_bytes=64) for g in range(2)]
-        ws = [keep.tile([P, 768], U8, name="ws%d" % g, align_bytes=64) for g in range(2)]
+        wc = [keep.tile([P, 832], U32, name="wc%d" % g, align_bytes=256)[:, 32:32 + 768] for g in range(2)]
+        ws = [keep.tile([P, 1024], U8, name="ws%d" % g, align_bytes=256)[:, 128:128 + 768] for g in range(2)]
         osb = [keep.tile([P, 4096], F32, name="osb%d" % m) for m in range(2)]
+        wsort = [osb[0][:, 1536 * g:1536 * (g + 1)].bitcast(BF16) for g in range(2)]
 
         scr = keep.tile([P, 2], F32, name="scr")
         nc.vector.memset(scr[:, 0:1], 0.0)
@@ -74,16 +80,17 @@ def tile_skeletonconv_t_kernel(tc, x, weight, dilation, step, out):
             for r in (1, 0):
                 lo = 2 * (FIRST[r] + PAIR * pi + 32)
                 nc.vector.memset(gf[:, :, lo:lo + 32 * 66].rearrange("p g (a c) -> p g a c", c=66)[:, :, :, 0:2], 0.0)
-        for c in (64, 1216):
-            nc.vector.memset(gf[:, :, 2 * c:2 * c + 2], 0.0)
-        for g in range(2):
-            for (c0, w) in ((0, 64), (3360, 32)):
-                nc.vector.memset(xc[g][:, c0:c0 + 1152 + w].bitcast(I32)[:, 0:w], 0)
-                nc.vector.memset(xc[g][:, c0 + 1152:c0 + 1152 + w].bitcast(I32), 0)
-                nc.vector.memset(xs[g][:, c0:c0 + w].bitcast(I32), 0)
-                nc.vector.memset(xs[g][:, c0 + 1152:c0 + 1152 + w].bitcast(I32), 0)
-            nc.vector.memset(lc[g][:, 0:64].bitcast(I32), 0)
-            nc.vector.memset(ls[g][:, 0:64].bitcast(I32), 0)
+        nc.vector.memset(
+            gf[:, :, 128:128 + 4608].rearrange("p g (b c) -> p g b c", b=2)[:, :, :, 0:2], 0.0
+        )
+        for t in (xc_all, xs_all):
+            tg = (xc_all[:] if t is xc_all else xs_all[:, 0:0 + 2 * XS]).bitcast(I32).rearrange("p (g c) -> p g c", g=2)
+            n = 4 if t is xs_all else 1
+            for (s0, lead, w) in ((0, 0, 64), (2240, 1120, 32)):
+                tb = tg[:, :, s0 // n:(s0 + 2 * PAIR) // n].rearrange("p g (b c) -> p g b c", b=2)
+                nc.vector.memset(tb[:, :, :, lead // n:(lead + w) // n], 0)
+        nc.vector.memset(lc_all[:].bitcast(I32).rearrange("p (g c) -> p g c", g=2)[:, :, 0:64], 0)
+        nc.vector.memset(ls_all[:].bitcast(I32).rearrange("p (g c) -> p g c", g=2)[:, :, 0:16], 0)
 
         wraw = {}
         raw = {}
@@ -126,10 +133,10 @@ def tile_skeletonconv_t_kernel(tc, x, weight, dilation, step, out):
                     in_=srcw.rearrange("o (p u e k) -> o u p e k", u=2, e=2, k=3)[:, u, p0:p1, :, :],
                 )
 
-        def wtrans(g, k):
+        def wtrans(g, k, ms=(0, 1)):
             wsf = wsort[g][:].bitcast(F32)
             bank = 3 * g + k
-            for m in range(2):
+            for m in ms:
                 for u in range(2):
                     nc.tensor.transpose(
                         ps[:, bank * 512 + m * 256 + u * P:bank * 512 + m * 256 + (u + 1) * P],
@@ -313,69 +320,67 @@ def tile_skeletonconv_t_kernel(tc, x, weight, dilation, step, out):
             pe(i, g, ((1, 0), (1, 2)), (1,))
             pe(i, g, ((0, 1),))
 
-        load_w(0, 0)
-        load_w(0, 1)
-        load_x(0, 0, 16, 32)
-        load_x(1, 0, 16, 32)
-        load_w(1, 0)
-        load_w(1, 1)
-        load_x(0, 0, 0, 16)
-        load_x(1, 0, 0, 16)
+        for g in range(2):
+            for m in range(2):
+                load_w(g, m)
+        for h0 in (16, 0):
+            for b in range(2):
+                load_x(b, 0, h0, h0 + 16)
         for (b, g) in ((0, 1), (1, 1), (2, 0), (3, 0), (2, 1), (3, 1)):
             load_x(b, g)
         idle(7)
-        PC = 48
+        PC = 16
         for m in range(2):
             wsrt(0, m, 0, 0, 128, "V")
             wsrt(0, m, 1, 0, PC, "V")
             wsrt(0, m, 1, PC, 128, "S")
         for k in (1, 2, 0):
             wtrans(0, k)
+        idle(2)
+        for m in range(2):
+            for u in range(2):
+                wsrt(1, m, u, 0, 128, "V")
+        for k in (1, 2, 0):
+            wout(0, k, "S")
+        for k in (1, 0, 2):
+            wtrans(1, k)
+        idle(4)
         rg(0, 0, 1, 0, 8, "V")
-        wout(0, 1, "S")
-        wout(0, 2, "S")
         wq(0, 256, 512)
         rg(1, 0, 1, 0, 8, "V")
         wq(0, 512, 768)
         qo(0, 0, 0)
-        wout(0, 0, "S")
-        rge(0, 0, 0)
-        idle(5)
-        pe(0, 0, A)
-        for m in range(2):
-            for u in range(2):
-                wsrt(1, m, u, 0, 128, "V")
-        for k in range(3):
-            wtrans(1, k)
-        rg(0, 0, 1, 8, 16, "V")
         wq(0, 0, 256)
+        pe(0, 0, A)
+        rge(0, 0, 0)
         qe(0, 0, 0)
         pe_b(0, 0)
-        rg(0, 0, 0, 8, 16, "S")
+        rg(0, 0, 1, 8, 16, "S")
         rg(1, 0, 1, 8, 16, "V")
         wout(1, 1, "S")
         wout(1, 0, "S")
-        wout(1, 2, "S")
+        rg(0, 0, 0, 8, 16, "S")
         rg(1, 0, 0, 8, 16, "S")
         qo(0, 0, 1)
+        wout(1, 2, "V")
         pe(0, 0, C)
         pe(1, 0, A)
         pe(1, 0, C)
-        rg(0, 1, 1, 0, 8, "V")
         wq(1, 256, 512)
+        rg(0, 1, 1, 0, 8, "V")
         qe(0, 0, 1)
         pe_b(1, 0)
         rge(0, 1, 0)
-        rg(0, 1, 1, 8, 16, "V")
         rg(1, 1, 1, 0, 8, "V")
         wq(1, 512, 768)
         qo(0, 1, 0)
         wq(1, 0, 256)
         pe(0, 1, A)
+        rg(0, 1, 1, 8, 16, "V")
         qe(0, 1, 0)
+        pe_b(0, 1)
         rg(1, 1, 1, 8, 16, "V")
         rge(0, 1, 1)
-        pe_b(0, 1)
         qo(0, 1, 1)
         pe(0, 1, C)
         pe(1, 1, A)

@@ -260,15 +260,20 @@ def tile_skeletonconv_t_kernel(tc, x, weight, dilation, step, out):
                 ps[:, col:col + P].rearrange("p (h b w) -> p b h w", h=2, b=2),
             )
 
-        def store(m, b0, b1, h0, h1):
+        def store(m, bs, h0, h1):
             nc.sync.dma_start(
-                out=out[b0:b1, m * P:(m + 1) * P, h0:h1, :].rearrange("b o h w -> o b (h w)"),
-                in_=osb[m][:].rearrange("p (b c) -> p b c", b=4)[:, b0:b1, 32 * h0:32 * h1],
+                out=out[bs, m * P:(m + 1) * P, h0:h1, :].rearrange("b o h w -> o b (h w)"),
+                in_=osb[m][:].rearrange("p (b c) -> p b c", b=4)[:, bs, 32 * h0:32 * h1],
             )
 
         def st(i, m):
             pi = WINDOWS[(i, m)][0]
-            store(m, 2 * pi, 2 * pi + 2, *STORES[(i, m)])
+            (h0, h1) = STORES[(i, m)]
+            if h0 == 2:
+                store(m, slice(2 * pi, 2 * pi + 1), 0, h1)
+                store(m, slice(2 * pi + 1, 2 * pi + 2), 2, h1)
+            else:
+                store(m, slice(2 * pi, 2 * pi + 2), h0, h1)
 
         def left(g):
             for (d, c0, lead) in ((64, 1087, 0), (128, 1088, 0), (192, 3327, 1120), (256, 3328, 1120), (320, 1023, 0)):
@@ -355,14 +360,14 @@ def tile_skeletonconv_t_kernel(tc, x, weight, dilation, step, out):
         rge(0, 0, 0)
         qe(0, 0, 0)
         pe_b(0, 0)
-        rg(0, 0, 1, 8, 16, "S")
+        rg(0, 0, 1, 8, 16, "V")
         rg(1, 0, 1, 8, 16, "V")
         wout(1, 1, "S")
         wout(1, 0, "S")
+        wout(1, 2, "S")
         rg(0, 0, 0, 8, 16, "S")
         rg(1, 0, 0, 8, 16, "S")
         qo(0, 0, 1)
-        wout(1, 2, "V")
         pe(0, 0, C)
         pe(1, 0, A)
         pe(1, 0, C)
@@ -407,7 +412,7 @@ def tile_skeletonconv_t_kernel(tc, x, weight, dilation, step, out):
         qe(1, 0, 0)
         dr(0, 1, 1, "V")
         st(1, 1)
-        rge(1, 0, 1, "VS")
+        rge(1, 0, 1, "VV")
         pe_b(2, 0)
         qo(1, 0, 1)
         pe(2, 0, C)
@@ -450,4 +455,4 @@ def tile_skeletonconv_t_kernel(tc, x, weight, dilation, step, out):
                     mml(m, g, k, c)
                     c += 1
             drl(m, "SV"[m])
-            store(m, 0, 4, 0, 2)
+            store(m, slice(1, 4, 2), 0, 2)

@@ -298,8 +298,6 @@ def tile_skeletonconv_t_kernel(tc, x, weight, dilation, step, out):
 
         def qe(pi, g, hh):
             q(g, *QE[(pi, hh)])
-            if hh:
-                q(g, QE[(pi, hh)][1], QE[(pi, hh)][1] + 32)
 
         def rgo(pi, g, h, engs="VV"):
             for e in range(2):
@@ -371,13 +369,12 @@ def tile_skeletonconv_t_kernel(tc, x, weight, dilation, step, out):
         pe(0, 0, C)
         pe(1, 0, A)
         pe(1, 0, C)
-        wq(1, 256, 512)
+        wq(1, 256, 768)
         rg(0, 1, 1, 0, 8, "V")
         qe(0, 0, 1)
         pe_b(1, 0)
         rge(0, 1, 0)
         rg(1, 1, 1, 0, 8, "V")
-        wq(1, 512, 768)
         qo(0, 1, 0)
         wq(1, 0, 256)
         pe(0, 1, A)
@@ -410,7 +407,7 @@ def tile_skeletonconv_t_kernel(tc, x, weight, dilation, step, out):
         st(1, 0)
         pe(2, 0, A)
         qe(1, 0, 0)
-        dr(0, 1, 1, "V")
+        dr(0, 1, 1, "S")
         st(1, 1)
         rge(1, 0, 1, "VV")
         pe_b(2, 0)
@@ -439,6 +436,9 @@ def tile_skeletonconv_t_kernel(tc, x, weight, dilation, step, out):
         st(2, 0)
         dr(0, 2, 1, "V")
         st(2, 1)
+        for g in range(2):
+            for pi in range(2):
+                q(g, QE[(pi, 1)][1], QE[(pi, 1)][1] + 32)
         left(0)
         left(1)
         for (i, m) in ((3, 0), (3, 1), (4, 1)):

@@ -169,15 +169,11 @@ def tile_skeletonconv_t_kernel(tc, x, weight, dilation, step, out):
             src = t[:, 0:128 * (h1 - h0)].rearrange("p (j a r w) -> p j a r w", j=4, r=2, w=32)[
                 :, :, down(15 - a0 - h0 // 2, n), r, :
             ]
-            if eng == "S":
-                nc.scalar.copy(
-                    out=dst.rearrange("p a (w j) -> p a w j", j=4), in_=src.rearrange("p j a w -> p a w j")
-                )
-            else:
-                nc.vector.tensor_copy(
-                    out=dst.rearrange("p a (c i j) -> p a c j i", i=4, j=4),
-                    in_=src.rearrange("p j a (c i) -> p a c j i", i=4),
-                )
+            copy_on(
+                eng,
+                dst.rearrange("p a (c i j) -> p a c j i", i=4, j=4),
+                src.rearrange("p j a (c i) -> p a c j i", i=4),
+            )
 
         def q(g, c0, c1):
             nc.vector.quantize_mx(
@@ -341,8 +337,10 @@ def tile_skeletonconv_t_kernel(tc, x, weight, dilation, step, out):
             wtrans(0, k)
         idle(2)
         for m in range(2):
-            for u in range(2):
-                wsrt(1, m, u, 0, 128, "V")
+            wsrt(1, m, 0, 0, 128, "V")
+            wsrt(1, m, 1, 0, (64, 128)[m], "V")
+            if m == 0:
+                wsrt(1, m, 1, 64, 128, "S")
         for k in (1, 2, 0):
             wout(0, k, "S")
         for k in (1, 0, 2):

from contextlib import ExitStack

import concourse.bass as bass
import concourse.mybir as mybir
import concourse.tile as tile
from concourse.masks import make_identity

FP8X4 = mybir.dt.float8_e4m3fn_x4
BF16 = mybir.dt.bfloat16
F32 = mybir.dt.float32
I32 = mybir.dt.int32
U32 = mybir.dt.uint32
U8 = mybir.dt.uint8

FLOPS = 2 * 4 * 1024 * 1024 * 256 * 3

P = 128
NCOL = 4544
XP = 4608
XS = 4544
FIRST = (65, 2304)
PAIR = 1152
WIN0 = (64, 2304)
WINDOWS = {(i, m): (i // 2, 512 * (i % 2), 512) for i in range(4) for m in range(2)}
WINDOWS[(3, 1)] = (1, 512, 256)
WINDOWS[(4, 1)] = (1, 768, 256)
STORES = {(i, m): ((18, 32), (2, 18))[i % 2] for i in range(4) for m in range(2)}
STORES[(3, 1)] = (10, 18)
STORES[(4, 1)] = (2, 10)
SHIFT = ((2304, 0, 2240), (-2240, 0, -2304))


def down(first, n):
    last = first - n
    return slice(first, last if last >= 0 else None, -1)


def tile_skeletonconv_t_kernel(tc, x, weight, dilation, step, out):
    nc = tc.nc
    assert dilation == 1 and step == 1
    with ExitStack() as ctx:
        keep = ctx.enter_context(tc.tile_pool(name="keep", bufs=1))
        rawp = ctx.enter_context(tc.tile_pool(name="rawp", bufs=7))
        psp = ctx.enter_context(tc.psum_pool(name="psp", bufs=1))
        ctx.enter_context(tc.manual_schedule())

        ident = keep.tile([P, P], F32, name="ident")
        make_identity(nc, ident[:])
        ps = psp.tile([P, 4096], F32, name="ps")

        grp_all = keep.tile([P, 2 * 4 * NCOL], BF16, name="grp_all", align_bytes=64)
        grp = [grp_all[:, g * 4 * NCOL:(g + 1) * 4 * NCOL] for g in range(2)]
        xc_all = keep.tile([P, 2 * XP], U32, name="xc_all", align_bytes=256)
        xs_all = keep.tile([P, 2 * XS + 0], U8, name="xs_all", align_bytes=256)
        xc = [xc_all[:, g * XP:g * XP + NCOL] for g in range(2)]
        xs = [xs_all[:, 0 + g * XS:0 + g * XS + NCOL] for g in range(2)]
        lc_all = keep.tile([P, 2 * 384], U32, name="lc_all", align_bytes=256)
        ls_all = keep.tile([P, 2 * 384], U8, name="ls_all", align_bytes=256)
        lc = [lc_all[:, g * 384:(g + 1) * 384] for g in range(2)]
        ls = [ls_all[:, g * 384:(g + 1) * 384] for g in range(2)]
        wgrp = [keep.tile([P, 3072], BF16, name="wgrp%d" % g, align_bytes=64) for g in range(2)]
        wc = [keep.tile([P, 832], U32, name="wc%d" % g, align_bytes=256)[:, 32:32 + 768] for g in range(2)]
        ws = [keep.tile([P, 1024], U8, name="ws%d" % g, align_bytes=256)[:, 128:128 + 768] for g in range(2)]
        osb = [keep.tile([P, 4096], F32, name="osb%d" % m) for m in range(2)]
        wsort = [osb[0][:, 1536 * g:1536 * (g + 1)].bitcast(BF16) for g in range(2)]

        scr = keep.tile([P, 2], F32, name="scr")
        nc.vector.memset(scr[:, 0:1], 0.0)
        nc.scalar.copy(out=scr[:, 1:2], in_=scr[:, 0:1])

        warm = osb[1][:, 0:256].bitcast(BF16)
        nc.vector.memset(osb[1][:, 0:256], 0.0)

        def idle(n):
            for t in range(n):
                nc.tensor.matmul(ps[:, 6 * 512:7 * 512], lhsT=warm[:, 0:P], rhs=warm, start=True, stop=True)

        gf = grp_all[:].bitcast(F32).rearrange("p (g c) -> p g c", g=2)
        for pi in range(2):
            for r in (1, 0):
                lo = 2 * (FIRST[r] + PAIR * pi + 32)
                nc.vector.memset(gf[:, :, lo:lo + 32 * 66].rearrange("p g (a c) -> p g a c", c=66)[:, :, :, 0:2], 0.0)
        nc.vector.memset(
            gf[:, :, 128:128 + 4608].rearrange("p g (b c) -> p g b c", b=2)[:, :, :, 0:2], 0.0
        )
        for t in (xc_all, xs_all):
            tg = (xc_all[:] if t is xc_all else xs_all[:, 0:0 + 2 * XS]).bitcast(I32).rearrange("p (g c) -> p g c", g=2)
            n = 4 if t is xs_all else 1
            for (s0, lead, w) in ((0, 0, 64), (2240, 1120, 32)):
                tb = tg[:, :, s0 // n:(s0 + 2 * PAIR) // n].rearrange("p g (b c) -> p g b c", b=2)
                nc.vector.memset(tb[:, :, :, lead // n:(lead + w) // n], 0)
        nc.vector.memset(lc_all[:].bitcast(I32).rearrange("p (g c) -> p g c", g=2)[:, :, 0:64], 0)
        nc.vector.memset(ls_all[:].bitcast(I32).rearrange("p (g c) -> p g c", g=2)[:, :, 0:16], 0)

        wraw = {}
        raw = {}

        def copy_on(eng, out, in_):
            if eng == "S":
                nc.scalar.copy(out=out, in_=in_)
            else:
                nc.vector.tensor_copy(out=out, in_=in_)

        def load_w(g, m):
            t = wraw.get(g)
            if t is None:
                t = rawp.tile([P, 4096], BF16, name="raw")
                wraw[g] = t
            nc.sync.dma_start(
                out=t[:, m * 1536:(m + 1) * 1536],
                in_=weight[m * P:(m + 1) * P, g * 512:(g + 1) * 512, :].rearrange("o c k -> o (c k)"),
            )

        def load_x(b, g, h0=0, h1=32):
            t = rawp.tile([P, 4096], BF16, name="raw")
            raw.setdefault((b, g), []).append((h0, h1, t))
            nc.sync.dma_start(
                out=t[:, 0:128 * (h1 - h0)].rearrange("p (j c) -> p j c", j=4),
                in_=x[b, g * 512:(g + 1) * 512, h0:h1, :].rearrange("(p j) h w -> p j (h w)", j=4),
            )

        def wsrt(g, m, u, p0, p1, eng):
            dstw = wsort[g][:, m * 1536:(m + 1) * 1536]
            srcw = wraw[g][:, m * 1536:(m + 1) * 1536]
            if eng == "S":
                nc.scalar.copy(
                    out=dstw.rearrange("o (k u p e) -> o u k p e", k=3, u=2, e=2)[:, u, :, p0:p1, :],
                    in_=srcw.rearrange("o (p u e k) -> o u k p e", u=2, e=2, k=3)[:, u, :, p0:p1, :],
                )
            else:
                nc.vector.tensor_copy(
                    out=dstw.rearrange("o (k u p e) -> o u p e k", k=3, u=2, e=2)[:, u, p0:p1, :, :],
                    in_=srcw.rearrange("o (p u e k) -> o u p e k", u=2, e=2, k=3)[:, u, p0:p1, :, :],
                )

        def wtrans(g, k, ms=(0, 1)):
            wsf = wsort[g][:].bitcast(F32)
            bank = 3 * g + k
            for m in ms:
                for u in range(2):
                    nc.tensor.transpose(
                        ps[:, bank * 512 + m * 256 + u * P:bank * 512 + m * 256 + (u + 1) * P],
                        wsf[:, (m * 3 + k) * 256 + u * P:(m * 3 + k) * 256 + (u + 1) * P],
                        ident[:],
                    )

        def wout(g, k, eng):
            wgf = wgrp[g][:].bitcast(F32)
            bank = 3 * g + k
            copy_on(
                eng,
                wgf[:, k * 512:(k + 1) * 512].rearrange("p (n o u) -> p n o u", n=2, u=2),
                ps[:, bank * 512:(bank + 1) * 512].rearrange("p (n u o) -> p n o u", n=2, u=2),
            )

        def wq(g, c0, c1):
            nc.vector.quantize_mx(
                out=wc[g][:, c0:c1].bitcast(FP8X4), scales=ws[g][:, c0:c1], in_=wgrp[g][:, 4 * c0:4 * c1]
            )

        def rg(b, g, r, a0, a1, eng):
            base = 4 * (FIRST[r] + PAIR * (b // 2) + 33 * (b % 2) + 66 * a0)
            n = a1 - a0
            if b % 2 == 0 or a1 < 16:
                dst = grp[g][:, base:base + 264 * n].rearrange("p (a c) -> p a c", c=264)[:, :, 0:128]
            else:
                dst = grp[g][:, base - 132:base - 132 + 264 * n].rearrange("p (a c) -> p a c", c=264)[:, :, 132:260]
            (h0, h1, t) = [e for e in raw[(b, g)] if e[0] <= 2 * (16 - a1) and 2 * (16 - a0) <= e[1]][0]
            src = t[:, 0:128 * (h1 - h0)].rearrange("p (j a r w) -> p j a r w", j=4, r=2, w=32)[
                :, :, down(15 - a0 - h0 // 2, n), r, :
            ]
            copy_on(
                eng,
                dst.rearrange("p a (c i j) -> p a c j i", i=4, j=4),
                src.rearrange("p j a (c i) -> p a c j i", i=4),
            )

        def q(g, c0, c1):
            nc.vector.quantize_mx(
                out=xc[g][:, c0:c1].bitcast(FP8X4), scales=xs[g][:, c0:c1], in_=grp[g][:, 4 * c0:4 * c1]
            )

        def bank_col(r, i, m):
            return ((6 + (i % 2) * 4 + 2 * m + 1 - r) % 8) * 512

        seen = {}

        def mm(r, i, m, g, k):
            (pi, off, n) = WINDOWS[(i, m)]
            s = WIN0[r] + PAIR * pi + off + SHIFT[r][k]
            qq = 2 * k + m
            c = seen.get((r, i, m), 0)
            seen[(r, i, m)] = c + 1
            col = bank_col(r, i, m)
            nc.tensor.matmul_mx(
                out=ps[:, col:col + n],
                lhsT=wc[g][:, qq * P:(qq + 1) * P].bitcast(FP8X4),
                lhsT_scale=ws[g][:, qq * P:(qq + 1) * P],
                rhs=xc[g][:, s:s + n].bitcast(FP8X4),
                rhs_scale=xs[g][:, s:s + n],
                start=c == 0,
                stop=c == 5,
            )

        def mml(m, g, k, c):
            col = bank_col(1, 5, m)
            qq = 2 * k + m
            nc.tensor.matmul_mx(
                out=ps[:, col:col + P],
                lhsT=wc[g][:, qq * P:(qq + 1) * P].bitcast(FP8X4),
                lhsT_scale=ws[g][:, qq * P:(qq + 1) * P],
                rhs=lc[g][:, k * P:(k + 1) * P].bitcast(FP8X4),
                rhs_scale=ls[g][:, k * P:(k + 1) * P],
                start=c == 0,
                stop=c == 5,
            )

        def dr(r, i, m, eng):
            (pi, off, n) = WINDOWS[(i, m)]
            ov = osb[m][:].rearrange("p (b a r w) -> p b a r w", b=4, a=16, r=2)
            lo = off + WIN0[r] - FIRST[r]
            j0 = bank_col(r, i, m) - lo

            def part(s, w0, w1):
                if w0 < w1:
                    copy_on(
                        eng,
                        ov[:, 2 * pi + s % 2, 15 - s // 2, r, w0:w1],
                        ps[:, j0 + 33 * s + w0:j0 + 33 * s + w1],
                    )

            first = max(lo, 0) // 33
            if lo > 33 * first:
                part(first, lo - 33 * first, 32)
                first += 1
            last = (lo + n - 32) // 33 + 1
            a0, a1 = (first + 1) // 2, last // 2
            if first % 2:
                part(first, 0, 32)
            copy_on(
                eng,
                ov[:, 2 * pi:2 * pi + 2, down(15 - a0, a1 - a0), r, :],
                ps[:, j0 + 66 * a0:j0 + 66 * a1].rearrange("p (a e c) -> p e a c", e=2, c=33)[:, :, :, 0:32],
            )
            if last % 2:
                part(last - 1, 0, 32)
            if last < 31:
                part(last, 0, lo + n - 33 * last)

        def drl(m, eng):
            col = bank_col(1, 5, m)
            ov = osb[m][:].rearrange("p (b h w) -> p b h w", b=4, w=32)
            copy_on(
                eng,
                ov[:, 1:4:2, 0:2, :],
                ps[:, col:col + P].rearrange("p (h b w) -> p b h w", h=2, b=2),
            )

        def store(m, bs, h0, h1):
            nc.sync.dma_start(
                out=out[bs, m * P:(m + 1) * P, h0:h1, :].rearrange("b o h w -> o b (h w)"),
                in_=osb[m][:].rearrange("p (b c) -> p b c", b=4)[:, bs, 32 * h0:32 * h1],
            )

        def st(i, m):
            pi = WINDOWS[(i, m)][0]
            (h0, h1) = STORES[(i, m)]
            if h0 == 2:
                store(m, slice(2 * pi, 2 * pi + 1), 0, h1)
                store(m, slice(2 * pi + 1, 2 * pi + 2), 2, h1)
            else:
                store(m, slice(2 * pi, 2 * pi + 2), h0, h1)

        def left(g):
            for (d, c0, lead) in ((64, 1087, 0), (128, 1088, 0), (192, 3327, 1120), (256, 3328, 1120), (320, 1023, 0)):
                s0 = c0 - lead
                nc.vector.tensor_copy(
                    out=lc[g][:, d:d + 64].bitcast(I32).rearrange("p (b w) -> p b w", b=2),
                    in_=xc[g][:, s0:s0 + 2304].bitcast(I32).rearrange("p (b c) -> p b c", b=2)[:, :, lead:lead + 32],
                )
                nc.vector.tensor_copy(
                    out=ls[g][:, d:d + 64].rearrange("p (b w) -> p b w", b=2),
                    in_=xs[g][:, s0:s0 + 2304].rearrange("p (b c) -> p b c", b=2)[:, :, lead:lead + 32],
                )

        QO = {(pi, hh): (2304 + PAIR * pi + 512 * hh, 2816 + PAIR * pi + 512 * hh) for pi in range(2) for hh in range(2)}
        QE = {(pi, hh): (64 + PAIR * pi + 512 * hh, 576 + PAIR * pi + 512 * hh) for pi in range(2) for hh in range(2)}
        ODD = ((1, 1), (0, 2), (0, 0))

        def qo(pi, g, hh):
            q(g, *QO[(pi, hh)])
            if hh:
                q(g, QO[(pi, hh)][1], QO[(pi, hh)][1] + 32)

        def qe(pi, g, hh):
            q(g, *QE[(pi, hh)])

        def rgo(pi, g, h, engs="VV"):
            for e in range(2):
                rg(2 * pi + e, g, 1, *AO[h], engs[e])

        def rge(pi, g, h, engs="SS"):
            for e in range(2):
                rg(2 * pi + e, g, 0, *AE[h], engs[e])

        AO = ((0, 8), (8, 16))
        AE = ((0, 8), (8, 16))

        def pe(i, g, rks, ms=(0, 1)):
            for (r, k) in rks:
                for m in ms:
                    mm(r, i, m, g, k)

        A = ((1, 1), (0, 2))
        C = ((0, 0),)

        def pe_b(i, g):
            pe(i, g, ((1, 0), (1, 2)), (0,))
            pe(i, g, ((1, 0), (1, 2)), (1,))
            pe(i, g, ((0, 1),))

        for g in range(2):
            for m in range(2):
                load_w(g, m)
        for h0 in (16, 0):
            for b in range(2):
                load_x(b, 0, h0, h0 + 16)
        for (b, g) in ((0, 1), (1, 1), (2, 0), (3, 0), (2, 1), (3, 1)):
            load_x(b, g)
        idle(7)
        PC = 16
        for m in range(2):
            wsrt(0, m, 0, 0, 128, "V")
            wsrt(0, m, 1, 0, PC, "V")
            wsrt(0, m, 1, PC, 128, "S")
        for k in (1, 2, 0):
            wtrans(0, k)
        idle(2)
        for m in range(2):
            wsrt(1, m, 0, 0, 128, "V")
            wsrt(1, m, 1, 0, (64, 128)[m], "V")
            if m == 0:
                wsrt(1, m, 1, 64, 128, "S")
        for k in (1, 2, 0):
            wout(0, k, "S")
        for k in (1, 0, 2):
            wtrans(1, k)
        idle(4)
        rg(0, 0, 1, 0, 8, "V")
        wq(0, 256, 512)
        rg(1, 0, 1, 0, 8, "V")
        wq(0, 512, 768)
        qo(0, 0, 0)
        wq(0, 0, 256)
        pe(0, 0, A)
        rge(0, 0, 0)
        qe(0, 0, 0)
        pe_b(0, 0)
        rg(0, 0, 1, 8, 16, "V")
        rg(1, 0, 1, 8, 16, "V")
        wout(1, 1, "S")
        wout(1, 0, "S")
        wout(1, 2, "S")
        rg(0, 0, 0, 8, 16, "S")
        rg(1, 0, 0, 8, 16, "S")
        qo(0, 0, 1)
        pe(0, 0, C)
        pe(1, 0, A)
        pe(1, 0, C)
        wq(1, 256, 768)
        rg(0, 1, 1, 0, 8, "V")
        qe(0, 0, 1)
        pe_b(1, 0)
        rge(0, 1, 0)
        rg(1, 1, 1, 0, 8, "V")
        qo(0, 1, 0)
        wq(1, 0, 256)
        pe(0, 1, A)
        rg(0, 1, 1, 8, 16, "V")
        qe(0, 1, 0)
        pe_b(0, 1)
        rg(1, 1, 1, 8, 16, "V")
        rge(0, 1, 1)
        qo(0, 1, 1)
        pe(0, 1, C)
        pe(1, 1, A)
        pe(1, 1, C)
        rge(1, 0, 0)
        rg(2, 0, 1, 0, 8, "V")
        qe(0, 1, 1)
        dr(1, 0, 0, "S")
        dr(1, 0, 1, "S")
        pe_b(1, 1)
        rg(3, 0, 1, 0, 8, "V")
        dr(0, 0, 0, "S")
        st(0, 0)
        dr(0, 0, 1, "S")
        st(0, 1)
        rg(2, 0, 1, 8, 16, "V")
        qo(1, 0, 0)
        dr(1, 1, 0, "S")
        dr(1, 1, 1, "S")
        rg(3, 0, 1, 8, 16, "V")
        dr(0, 1, 0, "S")
        st(1, 0)
        pe(2, 0, A)
        qe(1, 0, 0)
        dr(0, 1, 1, "S")
        st(1, 1)
        rge(1, 0, 1, "VV")
        pe_b(2, 0)
        qo(1, 0, 1)
        pe(2, 0, C)
        pe(3, 0, A)
        pe(3, 0, C)
        rg(2, 1, 1, 0, 8, "V")
        qe(1, 0, 1)
        rge(1, 1, 0)
        pe_b(3, 0)
        rg(3, 1, 1, 0, 8, "V")
        rg(2, 1, 1, 8, 16, "V")
        qo(1, 1, 0)
        pe(2, 1, A)
        rg(3, 1, 1, 8, 16, "V")
        qe(1, 1, 0)
        rge(1, 1, 1)
        qo(1, 1, 1)
        pe_b(2, 1)
        qe(1, 1, 1)
        dr(1, 2, 0, "S")
        dr(1, 2, 1, "V")
        pe(2, 1, C)
        dr(0, 2, 0, "S")
        st(2, 0)
        dr(0, 2, 1, "V")
        st(2, 1)
        for g in range(2):
            for pi in range(2):
                q(g, QE[(pi, 1)][1], QE[(pi, 1)][1] + 32)
        left(0)
        left(1)
        for (i, m) in ((3, 0), (3, 1), (4, 1)):
            for r in (1, 0):
                for g in range(2) if i == 4 else (1,):
                    for k in (1, 0, 2):
                        mm(r, i, m, g, k)
                dr(r, i, m, "SV"[m])
            st(i, m)
        for m in range(2):
            c = 0
            for g in range(2):
                for k in range(3):
                    mml(m, g, k, c)
                    c += 1
            drl(m, "SV"[m])
            store(m, slice(1, 4, 2), 0, 2)
